import numpy as np
import ml_dtypes


def mxq(x, axis, fmt="e4m3"):
    dtype, down = {"e4m3": (ml_dtypes.float8_e4m3fn, 7), "e5m2": (ml_dtypes.float8_e5m2, 14)}[fmt]
    v = np.moveaxis(np.asarray(x, np.float32).astype(ml_dtypes.bfloat16).astype(np.float64), axis, -1)
    blocks = v.reshape(v.shape[:-1] + (-1, 32))
    amax = np.abs(blocks).max(-1, keepdims=True)
    byte = np.maximum(np.where(amax > 0, np.frexp(amax)[1] - 1 + 127, 0) - down, 1)
    scale = np.exp2(byte - 127.0)
    codes = (blocks / scale).astype(np.float32).astype(dtype).astype(np.float64)
    return np.moveaxis((codes * scale).reshape(v.shape), -1, axis)


WIDE = False


def mx_kscale(k):
    if not WIDE:
        return np.ones(k)
    levels = np.array([10, -10, 5, -5, 0])
    a = np.random.permutation(np.resize(levels, k // 512 * 4)).reshape(k // 512, 4)
    idx = np.arange(k)
    return np.exp2(a[idx // 512, idx % 128 // 32])


BF16 = ml_dtypes.bfloat16


def bf(x):
    return np.asarray(x, np.float32).astype(BF16)


def f64(x):
    return np.asarray(x).astype(np.float64)


B, S, D, R = 4, 1024, 512, 4
GAMMA = 1.0


def setup_inputs():
    s = mx_kscale(D)
    p = np.random.standard_normal((R, D)) / np.sqrt(R * D)
    q = (np.random.standard_normal((B, S, R))[..., None] * p).sum(2) + np.random.standard_normal((B, S, D)) * 0.3 / np.sqrt(D)
    k = (np.random.standard_normal((B, S, R))[..., None] * p).sum(2) + np.random.standard_normal((B, S, D)) * 0.3 / np.sqrt(D)
    return {"q": bf(q), "k": bf(k), "x": bf(np.random.standard_normal((B, S, D)) * s),
            "Wv": bf(np.random.standard_normal((D, D)) * 0.125 * np.sqrt(S / D) / s[:, None]),
            "bv": bf(np.random.standard_normal(D) * 0.1)}


def reference(q, k, x, Wv, bv):
    q, k = f64(q), f64(k)
    v = (mxq(f64(x), 2, "e4m3") @ mxq(f64(Wv), 0, "e4m3")) + f64(bv)
    q_sq = np.sum(q * q, axis=-1)
    k_sq = np.sum(k * k, axis=-1)
    qk = mxq(q, 2, "e4m3") @ mxq(k.transpose(0, 2, 1), 1, "e4m3")
    dist_sq = q_sq[:, :, None] + k_sq[:, None, :] - 2.0 * qk
    scores = np.exp(-GAMMA * dist_sq)
    e = np.exp(scores - scores.max(-1, keepdims=True))
    return (mxq(e, 2, "e4m3") @ mxq(v, 1, "e4m3")) / e.sum(-1, keepdims=True)

@@ -1,0 +1,259 @@
+from contextlib import ExitStack
+
+import concourse.bass as bass
+import concourse.mybir as mybir
+import concourse.tile as tile
+from concourse.masks import make_identity
+
+F32 = mybir.dt.float32
+BF16 = mybir.dt.bfloat16
+U32 = mybir.dt.uint32
+U8 = mybir.dt.uint8
+FP8X4 = mybir.dt.float8_e4m3fn_x4
+ACT = mybir.ActivationFunctionType
+ALU = mybir.AluOpType
+
+B, S, D = 4, 1024, 512
+P = 128
+NT = S // P
+FLOPS = 2 * B * S * D * D + 2 * 2 * B * S * S * D
+
+
+def tile_selfattentionhybrid_pa_t_kernel(tc, q, k, x, Wv, bv, out):
+    nc = tc.nc
+    with ExitStack() as ctx:
+        const = ctx.enter_context(tc.tile_pool(name="const", bufs=1))
+        raw = ctx.enter_context(tc.tile_pool(name="raw", bufs=2))
+        grp = ctx.enter_context(tc.tile_pool(name="grp", bufs=3))
+        opnd = ctx.enter_context(tc.tile_pool(name="opnd", bufs=2))
+        work = ctx.enter_context(tc.tile_pool(name="work", bufs=3))
+        small = ctx.enter_context(tc.tile_pool(name="small", bufs=4))
+        ps_prep = ctx.enter_context(tc.psum_pool(name="ps_prep", bufs=2))
+        ps_qk = ctx.enter_context(tc.psum_pool(name="ps_qk", bufs=4))
+        ps_et = ctx.enter_context(tc.psum_pool(name="ps_et", bufs=1))
+        ps_o = ctx.enter_context(tc.psum_pool(name="ps_o", bufs=1))
+
+        ident_f = const.tile([P, P], F32, name="ident_f")
+        make_identity(nc, ident_f[:])
+        ident_b = const.tile([P, P], BF16, name="ident_b")
+        make_identity(nc, ident_b[:])
+        junk_f = const.tile([P, S], F32, name="junk_f")
+        junk_b = const.tile([P, D], BF16, name="junk_b")
+
+        wv_raw = const.tile([P, 4, D], BF16, name="wv_raw")
+        for u in range(2):
+            nc.sync.dma_start(
+                out=wv_raw[:, 2 * u : 2 * u + 2, :],
+                in_=Wv[256 * u : 256 * u + 256, :].rearrange("(r e) c -> r e c", e=2),
+            )
+        bv_b = const.tile([P, D], BF16, name="bv_b")
+        nc.gpsimd.dma_start(out=bv_b[:], in_=bv.partition_broadcast(P))
+        wv_g = const.tile([P, D, 4], BF16, name="wv_g", align_bytes=64)
+        wv_codes = const.tile([P, D], U32, name="wv_codes", align_bytes=64)
+        wv_scales = const.tile([P, D], U8, name="wv_scales", align_bytes=64)
+
+        state = {}
+
+        def load(b):
+            tiles = {}
+            for nm, src in (("k", k), ("q", q), ("x", x)):
+                t_sb = raw.tile([P, NT, D], BF16, name="raw_" + nm, tag="raw_" + nm)
+                nc.sync.dma_start(out=t_sb[:], in_=src[b].rearrange("(p n) f -> p n f", n=NT))
+                tiles[nm] = t_sb
+            state[("raw", b)] = tiles
+
+        def transpose_quantise(b, nm):
+            t_sb = state[("raw", b)][nm]
+            g = grp.tile([P, 4 * S], BF16, name="g_" + nm, tag="g", align_bytes=64)
+            g_f = g[:].bitcast(F32)
+            codes = opnd.tile([P, S], U32, name="c_" + nm, tag="c_" + nm, align_bytes=64)
+            scales = opnd.tile([P, S], U8, name="s_" + nm, tag="s_" + nm, align_bytes=64)
+            for h in range(4):
+                bank = ps_prep.tile([P, 2, 2, P], F32, name="tp", tag="prep")
+                for nn in range(2):
+                    words = t_sb[:, 2 * h + nn, :].bitcast(F32)
+                    for u in range(2):
+                        nc.tensor.transpose(bank[:, nn, u, :], words[:, P * u : P * u + P], ident_f[:])
+                nc.vector.tensor_copy(
+                    out=g_f[:, 512 * h : 512 * h + 512].rearrange("p (n r u) -> p n r u", n=2, u=2),
+                    in_=bank[:].rearrange("p n u r -> p n r u"),
+                )
+                if h % 2 == 1:
+                    hh = h // 2
+                    nc.vector.quantize_mx(
+                        out=codes[:, 512 * hh : 512 * hh + 512].bitcast(FP8X4),
+                        scales=scales[:, 512 * hh : 512 * hh + 512],
+                        in_=g[:, 2048 * hh : 2048 * hh + 2048],
+                    )
+            state[(nm, b)] = (codes, scales)
+
+        def norms(b, nm):
+            t_sb = state[("raw", b)][nm]
+            sq = opnd.tile([P, NT], F32, name="sq_" + nm, tag="sq_" + nm)
+            for n in range(NT):
+                nc.scalar.activation(
+                    out=junk_b[:], in_=t_sb[:, n, :], func=ACT.Square, accum_out=sq[:, n : n + 1]
+                )
+            return sq
+
+        def k_norms(b):
+            ksq = norms(b, "k")
+            kb = opnd.tile([P, S], F32, name="kb", tag="kb")
+            for hh in range(2):
+                bank = ps_prep.tile([P, 4, P], F32, name="kbp", tag="prep")
+                for nn in range(4):
+                    n = 4 * hh + nn
+                    nc.tensor.matmul(
+                        bank[:, nn, :],
+                        lhsT=ksq[:, n : n + 1].to_broadcast([P, P]),
+                        rhs=ident_f[:],
+                        start=True,
+                        stop=True,
+                    )
+                nc.scalar.activation(
+                    out=kb[:, 512 * hh : 512 * hh + 512],
+                    in_=bank[:].rearrange("p a c -> p (a c)"),
+                    func=ACT.Copy,
+                    scale=-0.5,
+                )
+            state[("kb", b)] = kb
+
+        def q_norms(b):
+            qsq = norms(b, "q")
+            nq = opnd.tile([P, NT], F32, name="nq", tag="nq")
+            nc.vector.tensor_scalar_mul(out=nq[:], in0=qsq[:], scalar1=-1.0)
+            state[("nq", b)] = nq
+
+        def values(b, g):
+            if g == 0:
+                v_g = opnd.tile([P, 2, D, 4], BF16, name="v_g", tag="v_g", align_bytes=64)
+                v_codes = opnd.tile([P, 2, D], U32, name="v_codes", tag="v_codes", align_bytes=64)
+                v_scales = opnd.tile([P, 2, D], U8, name="v_scales", tag="v_scales", align_bytes=64)
+                state[("v", b)] = (v_g, v_codes, v_scales)
+            v_g, v_codes, v_scales = state[("v", b)]
+            x_codes, x_scales = state[("x", b)]
+            for dc in range(4):
+                bank = ps_prep.tile([P, 4, P], F32, name="vp", tag="prep")
+                for t in range(4):
+                    c0 = 512 * g + P * t
+                    nc.tensor.matmul_mx(
+                        out=bank[:, t, :],
+                        lhsT=x_codes[:, c0 : c0 + P].bitcast(FP8X4),
+                        lhsT_scale=x_scales[:, c0 : c0 + P],
+                        rhs=wv_codes[:, P * dc : P * dc + P].bitcast(FP8X4),
+                        rhs_scale=wv_scales[:, P * dc : P * dc + P],
+                        start=True,
+                        stop=True,
+                    )
+                nc.vector.tensor_tensor(
+                    out=v_g[:, g, P * dc : P * dc + P, :],
+                    in0=bank[:].rearrange("p t d -> p d t"),
+                    in1=bv_b[:, P * dc : P * dc + P].unsqueeze(2).to_broadcast([P, P, 4]),
+                    op=ALU.add,
+                )
+            nc.vector.quantize_mx(
+                out=v_codes[:, g, :].bitcast(FP8X4),
+                scales=v_scales[:, g, :],
+                in_=v_g[:, g, :, :].rearrange("p d t -> p (d t)"),
+            )
+
+        def attention(b, n):
+            q_codes, q_scales = state[("q", b)]
+            k_codes, k_scales = state[("k", b)]
+            kb = state[("kb", b)]
+            nq = state[("nq", b)]
+            v_g, v_codes, v_scales = state[("v", b)]
+            th = work.tile([P, S], F32, name="th", tag="th")
+            for hh in range(2):
+                ps = ps_qk.tile([P, 512], F32, name="qk", tag="qk")
+                nc.tensor.matmul_mx(
+                    out=ps[:],
+                    lhsT=q_codes[:, P * n : P * n + P].bitcast(FP8X4),
+                    lhsT_scale=q_scales[:, P * n : P * n + P],
+                    rhs=k_codes[:, 512 * hh : 512 * hh + 512].bitcast(FP8X4),
+                    rhs_scale=k_scales[:, 512 * hh : 512 * hh + 512],
+                    start=True,
+                    stop=True,
+                )
+                nc.vector.tensor_tensor(
+                    out=th[:, 512 * hh : 512 * hh + 512],
+                    in0=ps[:],
+                    in1=kb[:, 512 * hh : 512 * hh + 512],
+                    op=ALU.add,
+                )
+            mx = small.tile([P, 1], F32, name="mx", tag="mx")
+            nc.vector.tensor_scalar(
+                out=junk_f[:], in0=th[:], scalar1=1.0, scalar2=None, op0=ALU.mult, op1=ALU.max, accum_out=mx[:]
+            )
+            sc = work.tile([P, S], F32, name="sc", tag="sc")
+            nc.scalar.activation(out=sc[:], in_=th[:], func=ACT.Exp, bias=nq[:, n : n + 1], scale=2.0)
+            m = small.tile([P, 1], F32, name="m", tag="m")
+            nc.scalar.activation(out=m[:], in_=mx[:], func=ACT.Exp, bias=nq[:, n : n + 1], scale=2.0)
+            negm = small.tile([P, 1], F32, name="negm", tag="negm")
+            nc.vector.tensor_scalar_mul(out=negm[:], in0=m[:], scalar1=-1.0)
+            e = work.tile([P, S], BF16, name="e", tag="e")
+            rs = small.tile([P, 1], F32, name="rs", tag="rs")
+            nc.scalar.activation(out=e[:], in_=sc[:], func=ACT.Exp, bias=negm[:], scale=1.0, accum_out=rs[:])
+            et = ps_et.tile([P, 2, 4, P], BF16, name="et", tag="et")
+            for g in range(2):
+                for t in range(4):
+                    c0 = 512 * g + P * t
+                    nc.tensor.transpose(et[:, g, t, :], e[:, c0 : c0 + P], ident_b[:])
+            e_g = work.tile([P, 2, P, 4], BF16, name="e_g", tag="e_g", align_bytes=64)
+            nc.scalar.copy(out=e_g[:], in_=et[:].rearrange("p g t i -> p g i t"))
+            e_codes = work.tile([P, 2 * P], U32, name="e_codes", tag="e_codes", align_bytes=64)
+            e_scales = work.tile([P, 2 * P], U8, name="e_scales", tag="e_scales", align_bytes=64)
+            nc.vector.quantize_mx(
+                out=e_codes[:].bitcast(FP8X4),
+                scales=e_scales[:],
+                in_=e_g[:].rearrange("p g i t -> p (g i t)"),
+            )
+            o_ps = ps_o.tile([P, D], F32, name="o_ps", tag="o")
+            for g in range(2):
+                nc.tensor.matmul_mx(
+                    out=o_ps[:],
+                    lhsT=e_codes[:, P * g : P * g + P].bitcast(FP8X4),
+                    lhsT_scale=e_scales[:, P * g : P * g + P],
+                    rhs=v_codes[:, g, :].bitcast(FP8X4),
+                    rhs_scale=v_scales[:, g, :],
+                    start=(g == 0),
+                    stop=(g == 1),
+                )
+            rinv = small.tile([P, 1], F32, name="rinv", tag="rinv")
+            nc.vector.reciprocal(out=rinv[:], in_=rs[:])
+            if n % 2 == 0:
+                state["o_sb"] = work.tile([P, 2, D], F32, name="o_sb", tag="o_sb")
+            o_sb = state["o_sb"]
+            nc.vector.tensor_scalar_mul(out=o_sb[:, n % 2, :], in0=o_ps[:], scalar1=rinv[:])
+            if n % 2 == 1:
+                nc.sync.dma_start(
+                    out=out[b].rearrange("(p n) d -> p n d", n=NT)[:, n - 1 : n + 1, :], in_=o_sb[:]
+                )
+
+        def prep_pieces(b):
+            return [
+                lambda: transpose_quantise(b, "k"),
+                lambda: k_norms(b),
+                lambda: transpose_quantise(b, "q"),
+                lambda: q_norms(b),
+                lambda: transpose_quantise(b, "x"),
+                lambda: values(b, 0),
+                lambda: values(b, 1),
+            ]
+
+        load(0)
+        nc.vector.tensor_copy(out=wv_g[:], in_=wv_raw[:].rearrange("p t c -> p c t"))
+        nc.vector.quantize_mx(
+            out=wv_codes[:].bitcast(FP8X4), scales=wv_scales[:], in_=wv_g[:].rearrange("p c t -> p (c t)")
+        )
+        load(1)
+        for piece in prep_pieces(0):
+            piece()
+        for b in range(B):
+            pieces = prep_pieces(b + 1) if b + 1 < B else []
+            for n in range(NT):
+                attention(b, n)
+                if n == 0 and b + 2 < B:
+                    load(b + 2)
+                if n < len(pieces):
+                    pieces[n]()

@@ -1,8 +1,6 @@
 from contextlib import ExitStack
 
-import concourse.bass as bass
 import concourse.mybir as mybir
-import concourse.tile as tile
 from concourse.masks import make_identity
 
 F32 = mybir.dt.float32
@@ -12,97 +10,85 @@ U8 = mybir.dt.uint8
 FP8X4 = mybir.dt.float8_e4m3fn_x4
 ACT = mybir.ActivationFunctionType
 ALU = mybir.AluOpType
+AX = mybir.AxisListType
 
 B, S, D = 4, 1024, 512
 P = 128
 NT = S // P
+STEPS = B * NT
 FLOPS = 2 * B * S * D * D + 2 * 2 * B * S * S * D
+
+UNITS = (
+    [(nm, h) for nm in ("k", "q", "x") for h in range(4)]
+    + [("kb", 0), ("kb", 1), None]
+    + [("v", j) for j in range(8)]
+    + [None]
+)
+PER_STEP = 3
 
 
 def tile_selfattentionhybrid_pa_t_kernel(tc, q, k, x, Wv, bv, out):
     nc = tc.nc
+    srcs = {"k": k, "q": q, "x": x}
     with ExitStack() as ctx:
         const = ctx.enter_context(tc.tile_pool(name="const", bufs=1))
         raw = ctx.enter_context(tc.tile_pool(name="raw", bufs=2))
         grp = ctx.enter_context(tc.tile_pool(name="grp", bufs=3))
         opnd = ctx.enter_context(tc.tile_pool(name="opnd", bufs=2))
-        work = ctx.enter_context(tc.tile_pool(name="work", bufs=3))
+        work = ctx.enter_context(tc.tile_pool(name="work", bufs=2))
+        outp = ctx.enter_context(tc.tile_pool(name="outp", bufs=3))
         small = ctx.enter_context(tc.tile_pool(name="small", bufs=4))
-        ps_prep = ctx.enter_context(tc.psum_pool(name="ps_prep", bufs=2))
-        ps_qk = ctx.enter_context(tc.psum_pool(name="ps_qk", bufs=4))
+        ps_prep = ctx.enter_context(tc.psum_pool(name="ps_prep", bufs=4))
+        ps_qk = ctx.enter_context(tc.psum_pool(name="ps_qk", bufs=2))
         ps_et = ctx.enter_context(tc.psum_pool(name="ps_et", bufs=1))
         ps_o = ctx.enter_context(tc.psum_pool(name="ps_o", bufs=1))
+        ctx.enter_context(tc.manual_schedule())
 
         ident_f = const.tile([P, P], F32, name="ident_f")
         make_identity(nc, ident_f[:])
         ident_b = const.tile([P, P], BF16, name="ident_b")
         make_identity(nc, ident_b[:])
-        junk_f = const.tile([P, S], F32, name="junk_f")
         junk_b = const.tile([P, D], BF16, name="junk_b")
-
         wv_raw = const.tile([P, 4, D], BF16, name="wv_raw")
-        for u in range(2):
-            nc.sync.dma_start(
-                out=wv_raw[:, 2 * u : 2 * u + 2, :],
-                in_=Wv[256 * u : 256 * u + 256, :].rearrange("(r e) c -> r e c", e=2),
-            )
         bv_b = const.tile([P, D], BF16, name="bv_b")
-        nc.gpsimd.dma_start(out=bv_b[:], in_=bv.partition_broadcast(P))
         wv_g = const.tile([P, D, 4], BF16, name="wv_g", align_bytes=64)
         wv_codes = const.tile([P, D], U32, name="wv_codes", align_bytes=64)
         wv_scales = const.tile([P, D], U8, name="wv_scales", align_bytes=64)
 
-        state = {}
+        st = {}
+        pending = []
 
         def load(b):
-            tiles = {}
-            for nm, src in (("k", k), ("q", q), ("x", x)):
+            for nm in ("k", "q", "x"):
                 t_sb = raw.tile([P, NT, D], BF16, name="raw_" + nm, tag="raw_" + nm)
-                nc.sync.dma_start(out=t_sb[:], in_=src[b].rearrange("(p n) f -> p n f", n=NT))
-                tiles[nm] = t_sb
-            state[("raw", b)] = tiles
-
-        def transpose_quantise(b, nm):
-            t_sb = state[("raw", b)][nm]
-            g = grp.tile([P, 4 * S], BF16, name="g_" + nm, tag="g", align_bytes=64)
-            g_f = g[:].bitcast(F32)
-            codes = opnd.tile([P, S], U32, name="c_" + nm, tag="c_" + nm, align_bytes=64)
-            scales = opnd.tile([P, S], U8, name="s_" + nm, tag="s_" + nm, align_bytes=64)
-            for h in range(4):
-                bank = ps_prep.tile([P, 2, 2, P], F32, name="tp", tag="prep")
-                for nn in range(2):
-                    words = t_sb[:, 2 * h + nn, :].bitcast(F32)
-                    for u in range(2):
-                        nc.tensor.transpose(bank[:, nn, u, :], words[:, P * u : P * u + P], ident_f[:])
-                nc.vector.tensor_copy(
-                    out=g_f[:, 512 * h : 512 * h + 512].rearrange("p (n r u) -> p n r u", n=2, u=2),
-                    in_=bank[:].rearrange("p n u r -> p n r u"),
-                )
-                if h % 2 == 1:
-                    hh = h // 2
-                    nc.vector.quantize_mx(
-                        out=codes[:, 512 * hh : 512 * hh + 512].bitcast(FP8X4),
-                        scales=scales[:, 512 * hh : 512 * hh + 512],
-                        in_=g[:, 2048 * hh : 2048 * hh + 2048],
+                view = srcs[nm][b].rearrange("(p n) f -> p n f", n=NT)
+                for half in range(2):
+                    nc.sync.dma_start(
+                        out=t_sb[:, 4 * half : 4 * half + 4, :], in_=view[:, 4 * half : 4 * half + 4, :]
                     )
-            state[(nm, b)] = (codes, scales)
+                st[("raw", nm, b)] = t_sb
 
-        def norms(b, nm):
-            t_sb = state[("raw", b)][nm]
-            sq = opnd.tile([P, NT], F32, name="sq_" + nm, tag="sq_" + nm)
-            for n in range(NT):
-                nc.scalar.activation(
-                    out=junk_b[:], in_=t_sb[:, n, :], func=ACT.Square, accum_out=sq[:, n : n + 1]
+        def load_weights():
+            for u in range(2):
+                nc.sync.dma_start(
+                    out=wv_raw[:, 2 * u : 2 * u + 2, :],
+                    in_=Wv[256 * u : 256 * u + 256, :].rearrange("(r e) c -> r e c", e=2),
                 )
-            return sq
+            nc.gpsimd.dma_start(out=bv_b[:], in_=bv.partition_broadcast(P))
 
-        def k_norms(b):
-            ksq = norms(b, "k")
-            kb = opnd.tile([P, S], F32, name="kb", tag="kb")
-            for hh in range(2):
+        def quantise_weights():
+            nc.vector.tensor_copy(out=wv_g[:], in_=wv_raw[:].rearrange("p t c -> p c t"))
+            nc.vector.quantize_mx(
+                out=wv_codes[:].bitcast(FP8X4), scales=wv_scales[:], in_=wv_g[:].rearrange("p c t -> p (c t)")
+            )
+
+        def fill(b, unit):
+            kind, j = unit
+            if kind == "kb":
                 bank = ps_prep.tile([P, 4, P], F32, name="kbp", tag="prep")
+                ksq = st[("sq", "k", b)]
                 for nn in range(4):
-                    n = 4 * hh + nn
+                    n = 4 * j + nn
                     nc.tensor.matmul(
                         bank[:, nn, :],
                         lhsT=ksq[:, n : n + 1].to_broadcast([P, P]),
@@ -110,30 +96,10 @@ def tile_selfattentionhybrid_pa_t_kernel(tc, q, k, x, Wv, bv, out):
                         start=True,
                         stop=True,
                     )
-                nc.scalar.activation(
-                    out=kb[:, 512 * hh : 512 * hh + 512],
-                    in_=bank[:].rearrange("p a c -> p (a c)"),
-                    func=ACT.Copy,
-                    scale=-0.5,
-                )
-            state[("kb", b)] = kb
-
-        def q_norms(b):
-            qsq = norms(b, "q")
-            nq = opnd.tile([P, NT], F32, name="nq", tag="nq")
-            nc.vector.tensor_scalar_mul(out=nq[:], in0=qsq[:], scalar1=-1.0)
-            state[("nq", b)] = nq
-
-        def values(b, g):
-            if g == 0:
-                v_g = opnd.tile([P, 2, D, 4], BF16, name="v_g", tag="v_g", align_bytes=64)
-                v_codes = opnd.tile([P, 2, D], U32, name="v_codes", tag="v_codes", align_bytes=64)
-                v_scales = opnd.tile([P, 2, D], U8, name="v_scales", tag="v_scales", align_bytes=64)
-                state[("v", b)] = (v_g, v_codes, v_scales)
-            v_g, v_codes, v_scales = state[("v", b)]
-            x_codes, x_scales = state[("x", b)]
-            for dc in range(4):
+            elif kind == "v":
                 bank = ps_prep.tile([P, 4, P], F32, name="vp", tag="prep")
+                g, dc = divmod(j, 4)
+                x_codes, x_scales = st[("mx", "x", b)]
                 for t in range(4):
                     c0 = 512 * g + P * t
                     nc.tensor.matmul_mx(
@@ -145,25 +111,95 @@ def tile_selfattentionhybrid_pa_t_kernel(tc, q, k, x, Wv, bv, out):
                         start=True,
                         stop=True,
                     )
+            else:
+                bank = ps_prep.tile([P, 2, 2, P], F32, name="tp", tag="prep")
+                t_sb = st[("raw", kind, b)]
+                for nn in range(2):
+                    words = t_sb[:, 2 * j + nn, :].bitcast(F32)
+                    for u in range(2):
+                        nc.tensor.transpose(bank[:, nn, u, :], words[:, P * u : P * u + P], ident_f[:])
+            st[("bank", b, unit)] = bank
+
+        def drain(b, unit, on_scalar):
+            kind, j = unit
+            bank = st[("bank", b, unit)]
+            if kind == "kb":
+                if j == 0:
+                    st[("kb", b)] = opnd.tile([P, S], F32, name="kb", tag="kb")
+                dst = st[("kb", b)][:, 512 * j : 512 * j + 512]
+                src = bank[:].rearrange("p a c -> p (a c)")
+                if on_scalar:
+                    nc.scalar.activation(out=dst, in_=src, func=ACT.Copy, scale=-0.5)
+                else:
+                    nc.vector.tensor_scalar_mul(out=dst, in0=src, scalar1=-0.5)
+            elif kind == "v":
+                g, dc = divmod(j, 4)
+                if j == 0:
+                    st[("vg", b)] = opnd.tile([P, 2, D, 4], BF16, name="v_g", tag="v_g", align_bytes=64)
+                    st[("mx", "v", b)] = (
+                        opnd.tile([P, 2, D], U32, name="v_codes", tag="v_codes", align_bytes=64),
+                        opnd.tile([P, 2, D], U8, name="v_scales", tag="v_scales", align_bytes=64),
+                    )
+                v_g = st[("vg", b)]
                 nc.vector.tensor_tensor(
                     out=v_g[:, g, P * dc : P * dc + P, :],
                     in0=bank[:].rearrange("p t d -> p d t"),
                     in1=bv_b[:, P * dc : P * dc + P].unsqueeze(2).to_broadcast([P, P, 4]),
                     op=ALU.add,
                 )
-            nc.vector.quantize_mx(
-                out=v_codes[:, g, :].bitcast(FP8X4),
-                scales=v_scales[:, g, :],
-                in_=v_g[:, g, :, :].rearrange("p d t -> p (d t)"),
-            )
+                if dc == 3:
+                    v_codes, v_scales = st[("mx", "v", b)]
+                    pending.append(
+                        (v_codes[:, g, :], v_scales[:, g, :], v_g[:, g, :, :].rearrange("p d t -> p (d t)"))
+                    )
+            else:
+                if j == 0:
+                    st[("g", kind, b)] = grp.tile([P, 4 * S], BF16, name="g_" + kind, tag="g", align_bytes=64)
+                    st[("mx", kind, b)] = (
+                        opnd.tile([P, S], U32, name="c_" + kind, tag="c_" + kind, align_bytes=64),
+                        opnd.tile([P, S], U8, name="s_" + kind, tag="s_" + kind, align_bytes=64),
+                    )
+                g_t = st[("g", kind, b)]
+                dst = g_t[:].bitcast(F32)[:, 512 * j : 512 * j + 512].rearrange("p (n r u) -> p n r u", n=2, u=2)
+                src = bank[:].rearrange("p n u r -> p n r u")
+                if on_scalar:
+                    nc.scalar.copy(out=dst, in_=src)
+                else:
+                    nc.vector.tensor_copy(out=dst, in_=src)
+                if j % 2 == 1:
+                    hh = j // 2
+                    codes, scales = st[("mx", kind, b)]
+                    pending.append(
+                        (
+                            codes[:, 512 * hh : 512 * hh + 512],
+                            scales[:, 512 * hh : 512 * hh + 512],
+                            g_t[:, 2048 * hh : 2048 * hh + 2048],
+                        )
+                    )
 
-        def attention(b, n):
-            q_codes, q_scales = state[("q", b)]
-            k_codes, k_scales = state[("k", b)]
-            kb = state[("kb", b)]
-            nq = state[("nq", b)]
-            v_g, v_codes, v_scales = state[("v", b)]
-            th = work.tile([P, S], F32, name="th", tag="th")
+        def quantise_pending():
+            for codes, scales, src in pending:
+                nc.vector.quantize_mx(out=codes.bitcast(FP8X4), scales=scales, in_=src)
+            pending[:] = []
+
+        def norm(b, i):
+            nm, n = ("k", "q")[i // NT], i % NT
+            if n == 0:
+                st[("sq", nm, b)] = opnd.tile([P, NT], F32, name="sq_" + nm, tag="sq_" + nm)
+            sq = st[("sq", nm, b)]
+            nc.scalar.activation(
+                out=junk_b[:], in_=st[("raw", nm, b)][:, n, :], func=ACT.Square, accum_out=sq[:, n : n + 1]
+            )
+            if i == 2 * NT - 1:
+                nq = opnd.tile([P, NT], F32, name="nq", tag="nq")
+                nc.scalar.activation(out=nq[:], in_=sq[:], func=ACT.Copy, scale=-1.0)
+                st[("nq", b)] = nq
+
+        def dots(s):
+            b, n = divmod(s, NT)
+            q_codes, q_scales = st[("mx", "q", b)]
+            k_codes, k_scales = st[("mx", "k", b)]
+            banks = []
             for hh in range(2):
                 ps = ps_qk.tile([P, 512], F32, name="qk", tag="qk")
                 nc.tensor.matmul_mx(
@@ -175,39 +211,72 @@ def tile_selfattentionhybrid_pa_t_kernel(tc, q, k, x, Wv, bv, out):
                     start=True,
                     stop=True,
                 )
+                banks.append(ps)
+            st[("qk", s)] = banks
+
+        def add_key_norms(s):
+            b, n = divmod(s, NT)
+            kb = st[("kb", b)]
+            th = work.tile([P, S], F32, name="th", tag="th")
+            for hh in range(2):
                 nc.vector.tensor_tensor(
                     out=th[:, 512 * hh : 512 * hh + 512],
-                    in0=ps[:],
+                    in0=st[("qk", s)][hh][:],
                     in1=kb[:, 512 * hh : 512 * hh + 512],
                     op=ALU.add,
                 )
-            mx = small.tile([P, 1], F32, name="mx", tag="mx")
-            nc.vector.tensor_scalar(
-                out=junk_f[:], in0=th[:], scalar1=1.0, scalar2=None, op0=ALU.mult, op1=ALU.max, accum_out=mx[:]
-            )
+            st[("th", s)] = th
+
+        def scores(s):
+            b, n = divmod(s, NT)
             sc = work.tile([P, S], F32, name="sc", tag="sc")
-            nc.scalar.activation(out=sc[:], in_=th[:], func=ACT.Exp, bias=nq[:, n : n + 1], scale=2.0)
-            m = small.tile([P, 1], F32, name="m", tag="m")
-            nc.scalar.activation(out=m[:], in_=mx[:], func=ACT.Exp, bias=nq[:, n : n + 1], scale=2.0)
+            nc.scalar.activation(
+                out=sc[:], in_=st[("th", s)][:], func=ACT.Exp, bias=st[("nq", b)][:, n : n + 1], scale=2.0
+            )
+            st[("sc", s)] = sc
+
+        def row_max(s):
             negm = small.tile([P, 1], F32, name="negm", tag="negm")
-            nc.vector.tensor_scalar_mul(out=negm[:], in0=m[:], scalar1=-1.0)
+            nc.vector.tensor_reduce(out=negm[:], in_=st[("sc", s)][:], axis=AX.X, op=ALU.max, negate=True)
+            st[("negm", s)] = negm
+
+        def weights(s):
             e = work.tile([P, S], BF16, name="e", tag="e")
             rs = small.tile([P, 1], F32, name="rs", tag="rs")
-            nc.scalar.activation(out=e[:], in_=sc[:], func=ACT.Exp, bias=negm[:], scale=1.0, accum_out=rs[:])
+            nc.scalar.activation(
+                out=e[:], in_=st[("sc", s)][:], func=ACT.Exp, bias=st[("negm", s)][:], scale=1.0, accum_out=rs[:]
+            )
+            st[("e", s)] = e
+            st[("rs", s)] = rs
+
+        def flip(s):
+            e = st[("e", s)]
             et = ps_et.tile([P, 2, 4, P], BF16, name="et", tag="et")
             for g in range(2):
                 for t in range(4):
                     c0 = 512 * g + P * t
                     nc.tensor.transpose(et[:, g, t, :], e[:, c0 : c0 + P], ident_b[:])
+            st[("et", s)] = et
+
+        def regroup(s):
             e_g = work.tile([P, 2, P, 4], BF16, name="e_g", tag="e_g", align_bytes=64)
-            nc.scalar.copy(out=e_g[:], in_=et[:].rearrange("p g t i -> p g i t"))
+            nc.scalar.copy(out=e_g[:], in_=st[("et", s)][:].rearrange("p g t i -> p g i t"))
+            st[("e_g", s)] = e_g
+
+        def quantise_weights_of(s):
             e_codes = work.tile([P, 2 * P], U32, name="e_codes", tag="e_codes", align_bytes=64)
             e_scales = work.tile([P, 2 * P], U8, name="e_scales", tag="e_scales", align_bytes=64)
             nc.vector.quantize_mx(
                 out=e_codes[:].bitcast(FP8X4),
                 scales=e_scales[:],
-                in_=e_g[:].rearrange("p g i t -> p (g i t)"),
+                in_=st[("e_g", s)][:].rearrange("p g i t -> p (g i t)"),
             )
+            st[("mx", "e", s)] = (e_codes, e_scales)
+
+        def mix(s):
+            b, n = divmod(s, NT)
+            e_codes, e_scales = st[("mx", "e", s)]
+            v_codes, v_scales = st[("mx", "v", b)]
             o_ps = ps_o.tile([P, D], F32, name="o_ps", tag="o")
             for g in range(2):
                 nc.tensor.matmul_mx(
@@ -219,41 +288,66 @@ def tile_selfattentionhybrid_pa_t_kernel(tc, q, k, x, Wv, bv, out):
                     start=(g == 0),
                     stop=(g == 1),
                 )
+            st[("o", s)] = o_ps
+
+        def finish(s):
+            b, n = divmod(s, NT)
             rinv = small.tile([P, 1], F32, name="rinv", tag="rinv")
-            nc.vector.reciprocal(out=rinv[:], in_=rs[:])
+            nc.vector.reciprocal(out=rinv[:], in_=st[("rs", s)][:])
             if n % 2 == 0:
-                state["o_sb"] = work.tile([P, 2, D], F32, name="o_sb", tag="o_sb")
-            o_sb = state["o_sb"]
-            nc.vector.tensor_scalar_mul(out=o_sb[:, n % 2, :], in0=o_ps[:], scalar1=rinv[:])
+                st["o_sb"] = outp.tile([P, 2, D], F32, name="o_sb", tag="o_sb")
+            o_sb = st["o_sb"]
+            nc.vector.tensor_scalar_mul(out=o_sb[:, n % 2, :], in0=st[("o", s)][:], scalar1=rinv[:])
             if n % 2 == 1:
                 nc.sync.dma_start(
                     out=out[b].rearrange("(p n) d -> p n d", n=NT)[:, n - 1 : n + 1, :], in_=o_sb[:]
                 )
 
-        def prep_pieces(b):
-            return [
-                lambda: transpose_quantise(b, "k"),
-                lambda: k_norms(b),
-                lambda: transpose_quantise(b, "q"),
-                lambda: q_norms(b),
-                lambda: transpose_quantise(b, "x"),
-                lambda: values(b, 0),
-                lambda: values(b, 1),
-            ]
+        def run(stage, s):
+            if 0 <= s < STEPS:
+                stage(s)
+
+        def drains_of(s):
+            b, n = divmod(s - 1, NT)
+            if not 0 <= b + 1 < B:
+                return []
+            return [(b + 1, PER_STEP * n + i, UNITS[PER_STEP * n + i]) for i in range(PER_STEP)]
+
+        def drain_one(s, item):
+            b, idx, unit = item
+            if unit is not None:
+                on_scalar = unit[0] != "v" and (idx % 2 == 1 if s < 0 else idx % 3 == 2)
+                drain(b, unit, on_scalar)
 
         load(0)
-        nc.vector.tensor_copy(out=wv_g[:], in_=wv_raw[:].rearrange("p t c -> p c t"))
-        nc.vector.quantize_mx(
-            out=wv_codes[:].bitcast(FP8X4), scales=wv_scales[:], in_=wv_g[:].rearrange("p c t -> p (c t)")
-        )
-        load(1)
-        for piece in prep_pieces(0):
-            piece()
-        for b in range(B):
-            pieces = prep_pieces(b + 1) if b + 1 < B else []
-            for n in range(NT):
-                attention(b, n)
-                if n == 0 and b + 2 < B:
-                    load(b + 2)
-                if n < len(pieces):
-                    pieces[n]()
+        load_weights()
+        for s in range(-NT, STEPS + 2):
+            b, n = divmod(s, NT)
+            if n == 0 and b + 2 < B:
+                load(b + 2)
+            run(dots, s + 1)
+            run(scores, s)
+            run(finish, s - 2)
+            todo = drains_of(s)
+            for item in todo[:2]:
+                drain_one(s, item)
+            if b + 1 < B:
+                for unit in UNITS[PER_STEP * n : PER_STEP * n + PER_STEP]:
+                    if unit is not None:
+                        fill(b + 1, unit)
+            run(row_max, s)
+            run(regroup, s - 1)
+            run(quantise_weights_of, s - 1)
+            if s == 4 - NT:
+                quantise_weights()
+            quantise_pending()
+            run(mix, s - 1)
+            if b + 1 < B:
+                norm(b + 1, 2 * n)
+            run(add_key_norms, s + 1)
+            run(weights, s)
+            run(flip, s)
+            if b + 1 < B:
+                norm(b + 1, 2 * n + 1)
+            for item in todo[2:]:
+                drain_one(s, item)

@@ -42,7 +42,6 @@ def tile_selfattentionhybrid_pa_t_kernel(tc, q, k, x, Wv, bv, out):
         ps_qk = ctx.enter_context(tc.psum_pool(name="ps_qk", bufs=2))
         ps_et = ctx.enter_context(tc.psum_pool(name="ps_et", bufs=1))
         ps_o = ctx.enter_context(tc.psum_pool(name="ps_o", bufs=1))
-        ctx.enter_context(tc.manual_schedule())
 
         ident_f = const.tile([P, P], F32, name="ident_f")
         make_identity(nc, ident_f[:])

@@ -35,13 +35,14 @@ def tile_selfattentionhybrid_pa_t_kernel(tc, q, k, x, Wv, bv, out):
         raw = ctx.enter_context(tc.tile_pool(name="raw", bufs=2))
         grp = ctx.enter_context(tc.tile_pool(name="grp", bufs=3))
         opnd = ctx.enter_context(tc.tile_pool(name="opnd", bufs=2))
-        work = ctx.enter_context(tc.tile_pool(name="work", bufs=2))
+        work = ctx.enter_context(tc.tile_pool(name="work", bufs=4))
         outp = ctx.enter_context(tc.tile_pool(name="outp", bufs=3))
         small = ctx.enter_context(tc.tile_pool(name="small", bufs=4))
         ps_prep = ctx.enter_context(tc.psum_pool(name="ps_prep", bufs=4))
         ps_qk = ctx.enter_context(tc.psum_pool(name="ps_qk", bufs=2))
         ps_et = ctx.enter_context(tc.psum_pool(name="ps_et", bufs=1))
         ps_o = ctx.enter_context(tc.psum_pool(name="ps_o", bufs=1))
+        ctx.enter_context(tc.manual_schedule())
 
         ident_f = const.tile([P, P], F32, name="ident_f")
         make_identity(nc, ident_f[:])
@@ -271,6 +272,9 @@ def tile_selfattentionhybrid_pa_t_kernel(tc, q, k, x, Wv, bv, out):
                 in_=st[("e_g", s)][:].rearrange("p g i t -> p (g i t)"),
             )
             st[("mx", "e", s)] = (e_codes, e_scales)
+            rinv = small.tile([P, 1], F32, name="rinv", tag="rinv")
+            nc.vector.reciprocal(out=rinv[:], in_=st[("rs", s)][:])
+            st[("rinv", s)] = rinv
 
         def mix(s):
             b, n = divmod(s, NT)
@@ -291,8 +295,7 @@ def tile_selfattentionhybrid_pa_t_kernel(tc, q, k, x, Wv, bv, out):
 
         def finish(s):
             b, n = divmod(s, NT)
-            rinv = small.tile([P, 1], F32, name="rinv", tag="rinv")
-            nc.vector.reciprocal(out=rinv[:], in_=st[("rs", s)][:])
+            rinv = st[("rinv", s)]
             if n % 2 == 0:
                 st["o_sb"] = outp.tile([P, 2, D], F32, name="o_sb", tag="o_sb")
             o_sb = st["o_sb"]
@@ -320,13 +323,13 @@ def tile_selfattentionhybrid_pa_t_kernel(tc, q, k, x, Wv, bv, out):
 
         load(0)
         load_weights()
-        for s in range(-NT, STEPS + 2):
+        for s in range(-NT, STEPS + 4):
             b, n = divmod(s, NT)
             if n == 0 and b + 2 < B:
                 load(b + 2)
-            run(dots, s + 1)
+            run(dots, s + 2)
             run(scores, s)
-            run(finish, s - 2)
+            run(finish, s - 4)
             todo = drains_of(s)
             for item in todo[:2]:
                 drain_one(s, item)
@@ -334,19 +337,19 @@ def tile_selfattentionhybrid_pa_t_kernel(tc, q, k, x, Wv, bv, out):
                 for unit in UNITS[PER_STEP * n : PER_STEP * n + PER_STEP]:
                     if unit is not None:
                         fill(b + 1, unit)
-            run(row_max, s)
-            run(regroup, s - 1)
-            run(quantise_weights_of, s - 1)
+            run(regroup, s - 2)
             if s == 4 - NT:
                 quantise_weights()
             quantise_pending()
-            run(mix, s - 1)
+            run(quantise_weights_of, s - 3)
+            run(mix, s - 3)
             if b + 1 < B:
                 norm(b + 1, 2 * n)
-            run(add_key_norms, s + 1)
-            run(weights, s)
-            run(flip, s)
+            run(add_key_norms, s + 2)
+            run(weights, s - 1)
+            run(flip, s - 1)
             if b + 1 < B:
                 norm(b + 1, 2 * n + 1)
             for item in todo[2:]:
                 drain_one(s, item)
+            run(row_max, s)

@@ -18,13 +18,11 @@ NT = S // P
 STEPS = B * NT
 FLOPS = 2 * B * S * D * D + 2 * 2 * B * S * S * D
 
-UNITS = (
-    [(nm, h) for nm in ("k", "q", "x") for h in range(4)]
-    + [("kb", 0), ("kb", 1), None]
-    + [("v", j) for j in range(8)]
-    + [None]
+OTHERS = (
+    [("k", h) for h in range(4)]
+    + [unit for pair in zip([("q", h) for h in range(4)], [("gram", 0), ("gram", 1), ("kb", 0), ("kb", 1)]) for unit in pair]
+    + [("x", h) for h in range(4)]
 )
-PER_STEP = 3
 
 
 def tile_selfattentionhybrid_pa_t_kernel(tc, q, k, x, Wv, bv, out):
@@ -49,6 +47,8 @@ def tile_selfattentionhybrid_pa_t_kernel(tc, q, k, x, Wv, bv, out):
         ident_b = const.tile([P, P], BF16, name="ident_b")
         make_identity(nc, ident_b[:])
         junk_b = const.tile([P, D], BF16, name="junk_b")
+        ones_f = const.tile([P, P], F32, name="ones_f")
+        nc.vector.memset(ones_f[:], 1.0)
         wv_raw = const.tile([P, 4, D], BF16, name="wv_raw")
         bv_b = const.tile([P, D], BF16, name="bv_b")
         wv_g = const.tile([P, D, 4], BF16, name="wv_g", align_bytes=64)
@@ -57,16 +57,18 @@ def tile_selfattentionhybrid_pa_t_kernel(tc, q, k, x, Wv, bv, out):
 
         st = {}
         pending = []
+        ready = []
 
-        def load(b):
-            for nm in ("k", "q", "x"):
-                t_sb = raw.tile([P, NT, D], BF16, name="raw_" + nm, tag="raw_" + nm)
+        def load(nm, b, halves=(0, 1)):
+            if b < B:
+                if halves[0] == 0:
+                    st[("raw", nm, b)] = raw.tile([P, NT, D], BF16, name="raw_" + nm, tag="raw_" + nm)
+                t_sb = st[("raw", nm, b)]
                 view = srcs[nm][b].rearrange("(p n) f -> p n f", n=NT)
-                for half in range(2):
+                for half in halves:
                     nc.sync.dma_start(
                         out=t_sb[:, 4 * half : 4 * half + 4, :], in_=view[:, 4 * half : 4 * half + 4, :]
                     )
-                st[("raw", nm, b)] = t_sb
 
         def load_weights():
             for u in range(2):
@@ -84,18 +86,28 @@ def tile_selfattentionhybrid_pa_t_kernel(tc, q, k, x, Wv, bv, out):
 
         def fill(b, unit):
             kind, j = unit
-            if kind == "kb":
-                bank = ps_prep.tile([P, 4, P], F32, name="kbp", tag="prep")
-                ksq = st[("sq", "k", b)]
+            if kind == "gram":
+                bank = ps_prep.tile([P, 4, P], F32, name="gp", tag="prep")
+                g_k = st[("g", "k", b)]
                 for nn in range(4):
-                    n = 4 * j + nn
-                    nc.tensor.matmul(
-                        bank[:, nn, :],
-                        lhsT=ksq[:, n : n + 1].to_broadcast([P, P]),
-                        rhs=ident_f[:],
-                        start=True,
-                        stop=True,
-                    )
+                    c0 = P * (4 * j + nn)
+                    for t in range(4):
+                        nc.tensor.matmul(
+                            bank[:, nn, :],
+                            lhsT=g_k[:, c0 : c0 + P, t],
+                            rhs=g_k[:, c0 : c0 + P, t],
+                            start=(t == 0),
+                            stop=(t == 3),
+                        )
+            elif kind == "kb":
+                bank = ps_prep.tile([P, 4, P], F32, name="kbp", tag="prep")
+                nc.tensor.matmul(
+                    bank[:].rearrange("p a c -> p (a c)"),
+                    lhsT=ones_f[:],
+                    rhs=st[("diag", b)][:, j, :],
+                    start=True,
+                    stop=True,
+                )
             elif kind == "v":
                 bank = ps_prep.tile([P, 4, P], F32, name="vp", tag="prep")
                 g, dc = divmod(j, 4)
@@ -123,7 +135,16 @@ def tile_selfattentionhybrid_pa_t_kernel(tc, q, k, x, Wv, bv, out):
         def drain(b, unit, on_scalar):
             kind, j = unit
             bank = st[("bank", b, unit)]
-            if kind == "kb":
+            if kind == "gram":
+                if j == 0:
+                    st[("diag", b)] = opnd.tile([P, 2, 512], F32, name="diag", tag="diag")
+                nc.vector.tensor_tensor(
+                    out=st[("diag", b)][:, j, :].rearrange("p (a c) -> p a c", a=4),
+                    in0=bank[:],
+                    in1=ident_f[:].unsqueeze(1).to_broadcast([P, 4, P]),
+                    op=ALU.mult,
+                )
+            elif kind == "kb":
                 if j == 0:
                     st[("kb", b)] = opnd.tile([P, S], F32, name="kb", tag="kb")
                 dst = st[("kb", b)][:, 512 * j : 512 * j + 512]
@@ -154,13 +175,13 @@ def tile_selfattentionhybrid_pa_t_kernel(tc, q, k, x, Wv, bv, out):
                     )
             else:
                 if j == 0:
-                    st[("g", kind, b)] = grp.tile([P, 4 * S], BF16, name="g_" + kind, tag="g", align_bytes=64)
+                    st[("g", kind, b)] = grp.tile([P, S, 4], BF16, name="g_" + kind, tag="g", align_bytes=64)
                     st[("mx", kind, b)] = (
                         opnd.tile([P, S], U32, name="c_" + kind, tag="c_" + kind, align_bytes=64),
                         opnd.tile([P, S], U8, name="s_" + kind, tag="s_" + kind, align_bytes=64),
                     )
                 g_t = st[("g", kind, b)]
-                dst = g_t[:].bitcast(F32)[:, 512 * j : 512 * j + 512].rearrange("p (n r u) -> p n r u", n=2, u=2)
+                dst = g_t[:].bitcast(F32)[:, 256 * j : 256 * j + 256, :].rearrange("p (n r) u -> p n r u", n=2)
                 src = bank[:].rearrange("p n u r -> p n r u")
                 if on_scalar:
                     nc.scalar.copy(out=dst, in_=src)
@@ -173,24 +194,23 @@ def tile_selfattentionhybrid_pa_t_kernel(tc, q, k, x, Wv, bv, out):
                         (
                             codes[:, 512 * hh : 512 * hh + 512],
                             scales[:, 512 * hh : 512 * hh + 512],
-                            g_t[:, 2048 * hh : 2048 * hh + 2048],
+                            g_t[:, 512 * hh : 512 * hh + 512, :].rearrange("p c t -> p (c t)"),
                         )
                     )
 
         def quantise_pending():
-            for codes, scales, src in pending:
+            for codes, scales, src in ready:
                 nc.vector.quantize_mx(out=codes.bitcast(FP8X4), scales=scales, in_=src)
-            pending[:] = []
+            ready[:] = []
 
-        def norm(b, i):
-            nm, n = ("k", "q")[i // NT], i % NT
+        def norm(b, n):
             if n == 0:
-                st[("sq", nm, b)] = opnd.tile([P, NT], F32, name="sq_" + nm, tag="sq_" + nm)
-            sq = st[("sq", nm, b)]
+                st[("sq", "q", b)] = opnd.tile([P, NT], F32, name="sq_q", tag="sq_q")
+            sq = st[("sq", "q", b)]
             nc.scalar.activation(
-                out=junk_b[:], in_=st[("raw", nm, b)][:, n, :], func=ACT.Square, accum_out=sq[:, n : n + 1]
+                out=junk_b[:], in_=st[("raw", "q", b)][:, n, :], func=ACT.Square, accum_out=sq[:, n : n + 1]
             )
-            if i == 2 * NT - 1:
+            if n == NT - 1:
                 nq = opnd.tile([P, NT], F32, name="nq", tag="nq")
                 nc.scalar.activation(out=nq[:], in_=sq[:], func=ACT.Copy, scale=-1.0)
                 st[("nq", b)] = nq
@@ -309,47 +329,69 @@ def tile_selfattentionhybrid_pa_t_kernel(tc, q, k, x, Wv, bv, out):
             if 0 <= s < STEPS:
                 stage(s)
 
-        def drains_of(s):
-            b, n = divmod(s - 1, NT)
-            if not 0 <= b + 1 < B:
+        def fills_of(s):
+            if s < START:
                 return []
-            return [(b + 1, PER_STEP * n + i, UNITS[PER_STEP * n + i]) for i in range(PER_STEP)]
-
-        def drain_one(s, item):
-            b, idx, unit = item
-            if unit is not None:
-                on_scalar = unit[0] != "v" and (idx % 2 == 1 if s < 0 else idx % 3 == 2)
-                drain(b, unit, on_scalar)
-
-        load(0)
-        load_weights()
-        for s in range(-NT, STEPS + 4):
             b, n = divmod(s, NT)
-            if n == 0 and b + 2 < B:
-                load(b + 2)
+            bv_, j = divmod(s - 2, NT)
+            units = [(bv_ + 1, ("v", j))]
+            for unit in OTHERS[2 * n : 2 * n + 2]:
+                units.append((b + 2 if unit[0] == "x" else b + 1, unit))
+            return [(bb, unit) for bb, unit in units if 0 <= bb < B]
+
+        START = -2
+        LAG = 3
+        load("k", 0)
+        load("q", 0, (0,))
+        load("x", 0)
+        load("q", 0, (1,))
+        load_weights()
+        load("x", 1)
+        load("k", 1)
+        load("q", 1)
+        first = (
+            [("k", h) for h in range(4)]
+            + [("gram", 0), ("q", 0), ("q", 1), ("gram", 1)]
+            + [("x", h) for h in range(4)]
+            + [("kb", 0), ("kb", 1), ("q", 2), ("q", 3)]
+            + [("v", j) for j in range(4)]
+        )
+        for i in range(len(first) + LAG):
+            ready.extend(pending)
+            pending[:] = []
+            if i >= LAG:
+                drain(0, first[i - LAG], first[i - LAG][0] in ("k", "q", "x"))
+            if i < len(first):
+                fill(0, first[i])
+            quantise_pending()
+            if i == 14:
+                quantise_weights()
+            if 6 <= i < 20 and i % 2 == 0:
+                norm(0, (i - 6) // 2)
+        load("x", 2)
+        for s in range(START, STEPS + 4):
+            b, n = divmod(s, NT)
+            if n == 0 and s >= 0:
+                load("k", b + 2)
+                load("q", b + 2)
+                load("x", b + 3)
+            ready.extend(pending)
+            pending[:] = []
             run(dots, s + 2)
             run(scores, s)
             run(finish, s - 4)
-            todo = drains_of(s)
-            for item in todo[:2]:
-                drain_one(s, item)
-            if b + 1 < B:
-                for unit in UNITS[PER_STEP * n : PER_STEP * n + PER_STEP]:
-                    if unit is not None:
-                        fill(b + 1, unit)
+            for bb, unit in fills_of(s - 1):
+                drain(bb, unit, unit in (("k", 0), ("k", 2), ("x", 0), ("x", 2)) or unit[0] == "q")
+            for bb, unit in fills_of(s):
+                fill(bb, unit)
             run(regroup, s - 2)
-            if s == 4 - NT:
-                quantise_weights()
             quantise_pending()
             run(quantise_weights_of, s - 3)
             run(mix, s - 3)
-            if b + 1 < B:
-                norm(b + 1, 2 * n)
             run(add_key_norms, s + 2)
             run(weights, s - 1)
             run(flip, s - 1)
-            if b + 1 < B:
-                norm(b + 1, 2 * n + 1)
-            for item in todo[2:]:
-                drain_one(s, item)
+            bq, m = divmod(s + 1, NT)
+            if 0 <= bq + 1 < B:
+                norm(bq + 1, m)
             run(row_max, s)

@@ -14,61 +14,72 @@ AX = mybir.AxisListType
 
 B, S, D = 4, 1024, 512
 P = 128
+PACK = 4
 NT = S // P
+BANK = 512
 STEPS = B * NT
 FLOPS = 2 * B * S * D * D + 2 * 2 * B * S * S * D
 
-OTHERS = (
-    [("k", h) for h in range(4)]
-    + [unit for pair in zip([("q", h) for h in range(4)], [("gram", 0), ("gram", 1), ("kb", 0), ("kb", 1)]) for unit in pair]
-    + [("x", h) for h in range(4)]
+KEY_NORMS = [("gram", 0), ("gram", 1), ("spread", 0), ("spread", 1)]
+PAIRS = (
+    [(("k", 0), ("k", 1)), (("k", 2), ("k", 3))]
+    + [(("q", h), KEY_NORMS[h]) for h in range(4)]
+    + [(("x", 0), ("x", 1)), (("x", 2), ("x", 3))]
 )
+PROLOGUE = (
+    [("k", h) for h in range(4)]
+    + [("gram", 0), ("q", 0), ("q", 1), ("gram", 1)]
+    + [("x", h) for h in range(4)]
+    + [("spread", 0), ("spread", 1), ("q", 2), ("q", 3)]
+    + [("v", j) for j in range(4)]
+)
+PROLOGUE_LAG = 3
+FIRST_STEP = -2
+V_SHIFT = 2
 
 
 def tile_selfattentionhybrid_pa_t_kernel(tc, q, k, x, Wv, bv, out):
     nc = tc.nc
-    srcs = {"k": k, "q": q, "x": x}
+    sources = {"k": k, "q": q, "x": x}
     with ExitStack() as ctx:
         const = ctx.enter_context(tc.tile_pool(name="const", bufs=1))
         raw = ctx.enter_context(tc.tile_pool(name="raw", bufs=2))
-        grp = ctx.enter_context(tc.tile_pool(name="grp", bufs=3))
         opnd = ctx.enter_context(tc.tile_pool(name="opnd", bufs=2))
+        grouped = ctx.enter_context(tc.tile_pool(name="grouped", bufs=3))
         work = ctx.enter_context(tc.tile_pool(name="work", bufs=4))
-        outp = ctx.enter_context(tc.tile_pool(name="outp", bufs=3))
         small = ctx.enter_context(tc.tile_pool(name="small", bufs=4))
-        ps_prep = ctx.enter_context(tc.psum_pool(name="ps_prep", bufs=4))
-        ps_qk = ctx.enter_context(tc.psum_pool(name="ps_qk", bufs=2))
-        ps_et = ctx.enter_context(tc.psum_pool(name="ps_et", bufs=1))
-        ps_o = ctx.enter_context(tc.psum_pool(name="ps_o", bufs=1))
+        stores = ctx.enter_context(tc.tile_pool(name="stores", bufs=3))
+        ps_dots = ctx.enter_context(tc.psum_pool(name="ps_dots", bufs=2))
+        ps_ring = ctx.enter_context(tc.psum_pool(name="ps_ring", bufs=6))
         ctx.enter_context(tc.manual_schedule())
 
         ident_f = const.tile([P, P], F32, name="ident_f")
         make_identity(nc, ident_f[:])
         ident_b = const.tile([P, P], BF16, name="ident_b")
         make_identity(nc, ident_b[:])
-        junk_b = const.tile([P, D], BF16, name="junk_b")
+        squares = const.tile([P, D], BF16, name="squares")
         ones_f = const.tile([P, P], F32, name="ones_f")
         nc.vector.memset(ones_f[:], 1.0)
-        wv_raw = const.tile([P, 4, D], BF16, name="wv_raw")
-        bv_b = const.tile([P, D], BF16, name="bv_b")
-        wv_g = const.tile([P, D, 4], BF16, name="wv_g", align_bytes=64)
+        wv_raw = const.tile([P, PACK, D], BF16, name="wv_raw")
+        bv_all = const.tile([P, D], BF16, name="bv_all")
+        wv_grouped = const.tile([P, D, PACK], BF16, name="wv_grouped", align_bytes=64)
         wv_codes = const.tile([P, D], U32, name="wv_codes", align_bytes=64)
         wv_scales = const.tile([P, D], U8, name="wv_scales", align_bytes=64)
 
-        st = {}
-        pending = []
+        live = {}
+        drained = []
         ready = []
 
-        def load(nm, b, halves=(0, 1)):
+
+        def load(name, b, halves=(0, 1)):
             if b < B:
                 if halves[0] == 0:
-                    st[("raw", nm, b)] = raw.tile([P, NT, D], BF16, name="raw_" + nm, tag="raw_" + nm)
-                t_sb = st[("raw", nm, b)]
-                view = srcs[nm][b].rearrange("(p n) f -> p n f", n=NT)
+                    live[("raw", name, b)] = raw.tile([P, NT, D], BF16, name="raw_" + name, tag="raw_" + name)
+                rows = live[("raw", name, b)]
+                view = sources[name][b].rearrange("(p n) f -> p n f", n=NT)
                 for half in halves:
-                    nc.sync.dma_start(
-                        out=t_sb[:, 4 * half : 4 * half + 4, :], in_=view[:, 4 * half : 4 * half + 4, :]
-                    )
+                    tiles = slice(NT // 2 * half, NT // 2 * (half + 1))
+                    nc.sync.dma_start(out=rows[:, tiles, :], in_=view[:, tiles, :])
 
         def load_weights():
             for u in range(2):
@@ -76,78 +87,74 @@ def tile_selfattentionhybrid_pa_t_kernel(tc, q, k, x, Wv, bv, out):
                     out=wv_raw[:, 2 * u : 2 * u + 2, :],
                     in_=Wv[256 * u : 256 * u + 256, :].rearrange("(r e) c -> r e c", e=2),
                 )
-            nc.gpsimd.dma_start(out=bv_b[:], in_=bv.partition_broadcast(P))
+            nc.gpsimd.dma_start(out=bv_all[:], in_=bv.partition_broadcast(P))
 
         def quantise_weights():
-            nc.vector.tensor_copy(out=wv_g[:], in_=wv_raw[:].rearrange("p t c -> p c t"))
+            nc.vector.tensor_copy(out=wv_grouped[:], in_=wv_raw[:].rearrange("p t c -> p c t"))
             nc.vector.quantize_mx(
-                out=wv_codes[:].bitcast(FP8X4), scales=wv_scales[:], in_=wv_g[:].rearrange("p c t -> p (c t)")
+                out=wv_codes[:].bitcast(FP8X4),
+                scales=wv_scales[:],
+                in_=wv_grouped[:].rearrange("p c t -> p (c t)"),
             )
+
 
         def fill(b, unit):
             kind, j = unit
+            bank = ps_ring.tile([P, 4, P], F32, name="bank", tag="ring")
             if kind == "gram":
-                bank = ps_prep.tile([P, 4, P], F32, name="gp", tag="prep")
-                g_k = st[("g", "k", b)]
-                for nn in range(4):
-                    c0 = P * (4 * j + nn)
-                    for t in range(4):
+                k_t = live[("grouped", "k", b)]
+                for i in range(4):
+                    cols = slice(P * (4 * j + i), P * (4 * j + i + 1))
+                    for t in range(PACK):
                         nc.tensor.matmul(
-                            bank[:, nn, :],
-                            lhsT=g_k[:, c0 : c0 + P, t],
-                            rhs=g_k[:, c0 : c0 + P, t],
-                            start=(t == 0),
-                            stop=(t == 3),
+                            bank[:, i, :], lhsT=k_t[:, cols, t], rhs=k_t[:, cols, t], start=(t == 0), stop=(t == PACK - 1)
                         )
-            elif kind == "kb":
-                bank = ps_prep.tile([P, 4, P], F32, name="kbp", tag="prep")
+            elif kind == "spread":
                 nc.tensor.matmul(
                     bank[:].rearrange("p a c -> p (a c)"),
                     lhsT=ones_f[:],
-                    rhs=st[("diag", b)][:, j, :],
+                    rhs=live[("diagonal", b)][:, j, :],
                     start=True,
                     stop=True,
                 )
             elif kind == "v":
-                bank = ps_prep.tile([P, 4, P], F32, name="vp", tag="prep")
                 g, dc = divmod(j, 4)
-                x_codes, x_scales = st[("mx", "x", b)]
-                for t in range(4):
-                    c0 = 512 * g + P * t
+                x_codes, x_scales = live[("mx", "x", b)]
+                for t in range(PACK):
+                    keys = slice(BANK * g + P * t, BANK * g + P * (t + 1))
                     nc.tensor.matmul_mx(
                         out=bank[:, t, :],
-                        lhsT=x_codes[:, c0 : c0 + P].bitcast(FP8X4),
-                        lhsT_scale=x_scales[:, c0 : c0 + P],
-                        rhs=wv_codes[:, P * dc : P * dc + P].bitcast(FP8X4),
-                        rhs_scale=wv_scales[:, P * dc : P * dc + P],
+                        lhsT=x_codes[:, keys].bitcast(FP8X4),
+                        lhsT_scale=x_scales[:, keys],
+                        rhs=wv_codes[:, P * dc : P * (dc + 1)].bitcast(FP8X4),
+                        rhs_scale=wv_scales[:, P * dc : P * (dc + 1)],
                         start=True,
                         stop=True,
                     )
             else:
-                bank = ps_prep.tile([P, 2, 2, P], F32, name="tp", tag="prep")
-                t_sb = st[("raw", kind, b)]
-                for nn in range(2):
-                    words = t_sb[:, 2 * j + nn, :].bitcast(F32)
+                rows = live[("raw", kind, b)]
+                for i in range(2):
+                    words = rows[:, 2 * j + i, :].bitcast(F32)
                     for u in range(2):
-                        nc.tensor.transpose(bank[:, nn, u, :], words[:, P * u : P * u + P], ident_f[:])
-            st[("bank", b, unit)] = bank
+                        nc.tensor.transpose(bank[:, 2 * i + u, :], words[:, P * u : P * (u + 1)], ident_f[:])
+            live[("bank", b, unit)] = bank
 
         def drain(b, unit, on_scalar):
             kind, j = unit
-            bank = st[("bank", b, unit)]
+            bank = live[("bank", b, unit)]
             if kind == "gram":
                 if j == 0:
-                    st[("diag", b)] = opnd.tile([P, 2, 512], F32, name="diag", tag="diag")
+                    live[("diagonal", b)] = opnd.tile([P, 2, BANK], F32, name="diagonal", tag="diagonal")
                 nc.vector.tensor_tensor(
-                    out=st[("diag", b)][:, j, :].rearrange("p (a c) -> p a c", a=4),
+                    out=live[("diagonal", b)][:, j, :].rearrange("p (a c) -> p a c", a=4),
                     in0=bank[:],
                     in1=ident_f[:].unsqueeze(1).to_broadcast([P, 4, P]),
                     op=ALU.mult,
                 )
-            elif kind == "kb":
+            elif kind == "spread":
                 if j == 0:
-                    st[("kb", b)] = opnd.tile([P, S], F32, name="kb", tag="kb")
-                dst = st[("kb", b)][:, 512 * j : 512 * j + 512]
+                    live[("key_norms", b)] = opnd.tile([P, S], F32, name="key_norms", tag="key_norms")
+                dst = live[("key_norms", b)][:, BANK * j : BANK * (j + 1)]
                 src = bank[:].rearrange("p a c -> p (a c)")
                 if on_scalar:
                     nc.scalar.activation(out=dst, in_=src, func=ACT.Copy, scale=-0.5)
@@ -156,191 +163,175 @@ def tile_selfattentionhybrid_pa_t_kernel(tc, q, k, x, Wv, bv, out):
             elif kind == "v":
                 g, dc = divmod(j, 4)
                 if j == 0:
-                    st[("vg", b)] = opnd.tile([P, 2, D, 4], BF16, name="v_g", tag="v_g", align_bytes=64)
-                    st[("mx", "v", b)] = (
+                    live[("grouped", "v", b)] = opnd.tile([P, 2, D, PACK], BF16, name="v_grouped", tag="v_grouped", align_bytes=64)
+                    live[("mx", "v", b)] = (
                         opnd.tile([P, 2, D], U32, name="v_codes", tag="v_codes", align_bytes=64),
                         opnd.tile([P, 2, D], U8, name="v_scales", tag="v_scales", align_bytes=64),
                     )
-                v_g = st[("vg", b)]
+                v_grouped = live[("grouped", "v", b)]
                 nc.vector.tensor_tensor(
-                    out=v_g[:, g, P * dc : P * dc + P, :],
+                    out=v_grouped[:, g, P * dc : P * (dc + 1), :],
                     in0=bank[:].rearrange("p t d -> p d t"),
-                    in1=bv_b[:, P * dc : P * dc + P].unsqueeze(2).to_broadcast([P, P, 4]),
+                    in1=bv_all[:, P * dc : P * (dc + 1)].unsqueeze(2).to_broadcast([P, P, PACK]),
                     op=ALU.add,
                 )
                 if dc == 3:
-                    v_codes, v_scales = st[("mx", "v", b)]
-                    pending.append(
-                        (v_codes[:, g, :], v_scales[:, g, :], v_g[:, g, :, :].rearrange("p d t -> p (d t)"))
+                    v_codes, v_scales = live[("mx", "v", b)]
+                    drained.append(
+                        (v_codes[:, g, :], v_scales[:, g, :], v_grouped[:, g, :, :].rearrange("p d t -> p (d t)"))
                     )
             else:
                 if j == 0:
-                    st[("g", kind, b)] = grp.tile([P, S, 4], BF16, name="g_" + kind, tag="g", align_bytes=64)
-                    st[("mx", kind, b)] = (
-                        opnd.tile([P, S], U32, name="c_" + kind, tag="c_" + kind, align_bytes=64),
-                        opnd.tile([P, S], U8, name="s_" + kind, tag="s_" + kind, align_bytes=64),
+                    live[("grouped", kind, b)] = grouped.tile([P, S, PACK], BF16, name="grouped_" + kind, tag="grouped", align_bytes=64)
+                    live[("mx", kind, b)] = (
+                        opnd.tile([P, S], U32, name="codes_" + kind, tag="codes_" + kind, align_bytes=64),
+                        opnd.tile([P, S], U8, name="scales_" + kind, tag="scales_" + kind, align_bytes=64),
                     )
-                g_t = st[("g", kind, b)]
-                dst = g_t[:].bitcast(F32)[:, 256 * j : 256 * j + 256, :].rearrange("p (n r) u -> p n r u", n=2)
-                src = bank[:].rearrange("p n u r -> p n r u")
+                tokens = live[("grouped", kind, b)]
+                dst = tokens[:].bitcast(F32)[:, 2 * P * j : 2 * P * (j + 1), :].rearrange("p (i r) u -> p i r u", i=2)
+                src = bank[:].rearrange("p (i u) r -> p i r u", u=2)
                 if on_scalar:
                     nc.scalar.copy(out=dst, in_=src)
                 else:
                     nc.vector.tensor_copy(out=dst, in_=src)
                 if j % 2 == 1:
-                    hh = j // 2
-                    codes, scales = st[("mx", kind, b)]
-                    pending.append(
-                        (
-                            codes[:, 512 * hh : 512 * hh + 512],
-                            scales[:, 512 * hh : 512 * hh + 512],
-                            g_t[:, 512 * hh : 512 * hh + 512, :].rearrange("p c t -> p (c t)"),
-                        )
-                    )
+                    half = slice(BANK * (j // 2), BANK * (j // 2 + 1))
+                    codes, scales = live[("mx", kind, b)]
+                    drained.append((codes[:, half], scales[:, half], tokens[:, half, :].rearrange("p c t -> p (c t)")))
 
-        def quantise_pending():
+        def next_round():
+            ready.extend(drained)
+            drained[:] = []
+
+        def quantise_ready():
             for codes, scales, src in ready:
                 nc.vector.quantize_mx(out=codes.bitcast(FP8X4), scales=scales, in_=src)
             ready[:] = []
 
-        def norm(b, n):
+        def query_norms(b, n):
             if n == 0:
-                st[("sq", "q", b)] = opnd.tile([P, NT], F32, name="sq_q", tag="sq_q")
-            sq = st[("sq", "q", b)]
+                live[("sums", b)] = opnd.tile([P, NT], F32, name="sums", tag="sums")
+            sums = live[("sums", b)]
             nc.scalar.activation(
-                out=junk_b[:], in_=st[("raw", "q", b)][:, n, :], func=ACT.Square, accum_out=sq[:, n : n + 1]
+                out=squares[:], in_=live[("raw", "q", b)][:, n, :], func=ACT.Square, accum_out=sums[:, n : n + 1]
             )
             if n == NT - 1:
-                nq = opnd.tile([P, NT], F32, name="nq", tag="nq")
-                nc.scalar.activation(out=nq[:], in_=sq[:], func=ACT.Copy, scale=-1.0)
-                st[("nq", b)] = nq
+                negated = opnd.tile([P, NT], F32, name="negated", tag="negated")
+                nc.scalar.activation(out=negated[:], in_=sums[:], func=ACT.Copy, scale=-1.0)
+                live[("query_norms", b)] = negated
+
 
         def dots(s):
             b, n = divmod(s, NT)
-            q_codes, q_scales = st[("mx", "q", b)]
-            k_codes, k_scales = st[("mx", "k", b)]
+            q_codes, q_scales = live[("mx", "q", b)]
+            k_codes, k_scales = live[("mx", "k", b)]
             banks = []
-            for hh in range(2):
-                ps = ps_qk.tile([P, 512], F32, name="qk", tag="qk")
+            for h in range(2):
+                bank = ps_dots.tile([P, BANK], F32, name="dots", tag="dots")
                 nc.tensor.matmul_mx(
-                    out=ps[:],
-                    lhsT=q_codes[:, P * n : P * n + P].bitcast(FP8X4),
-                    lhsT_scale=q_scales[:, P * n : P * n + P],
-                    rhs=k_codes[:, 512 * hh : 512 * hh + 512].bitcast(FP8X4),
-                    rhs_scale=k_scales[:, 512 * hh : 512 * hh + 512],
+                    out=bank[:],
+                    lhsT=q_codes[:, P * n : P * (n + 1)].bitcast(FP8X4),
+                    lhsT_scale=q_scales[:, P * n : P * (n + 1)],
+                    rhs=k_codes[:, BANK * h : BANK * (h + 1)].bitcast(FP8X4),
+                    rhs_scale=k_scales[:, BANK * h : BANK * (h + 1)],
                     start=True,
                     stop=True,
                 )
-                banks.append(ps)
-            st[("qk", s)] = banks
+                banks.append(bank)
+            live[("dots", s)] = banks
 
         def add_key_norms(s):
-            b, n = divmod(s, NT)
-            kb = st[("kb", b)]
-            th = work.tile([P, S], F32, name="th", tag="th")
-            for hh in range(2):
-                nc.vector.tensor_tensor(
-                    out=th[:, 512 * hh : 512 * hh + 512],
-                    in0=st[("qk", s)][hh][:],
-                    in1=kb[:, 512 * hh : 512 * hh + 512],
-                    op=ALU.add,
-                )
-            st[("th", s)] = th
+            key_norms = live[("key_norms", s // NT)]
+            half_d = work.tile([P, S], F32, name="half_d", tag="half_d")
+            for h in range(2):
+                cols = slice(BANK * h, BANK * (h + 1))
+                nc.vector.tensor_tensor(out=half_d[:, cols], in0=live[("dots", s)][h][:], in1=key_norms[:, cols], op=ALU.add)
+            live[("half_d", s)] = half_d
 
         def scores(s):
             b, n = divmod(s, NT)
             sc = work.tile([P, S], F32, name="sc", tag="sc")
             nc.scalar.activation(
-                out=sc[:], in_=st[("th", s)][:], func=ACT.Exp, bias=st[("nq", b)][:, n : n + 1], scale=2.0
+                out=sc[:], in_=live[("half_d", s)][:], func=ACT.Exp, bias=live[("query_norms", b)][:, n : n + 1], scale=2.0
             )
-            st[("sc", s)] = sc
+            live[("scores", s)] = sc
 
         def row_max(s):
-            negm = small.tile([P, 1], F32, name="negm", tag="negm")
-            nc.vector.tensor_reduce(out=negm[:], in_=st[("sc", s)][:], axis=AX.X, op=ALU.max, negate=True)
-            st[("negm", s)] = negm
+            neg_max = small.tile([P, 1], F32, name="neg_max", tag="neg_max")
+            nc.vector.tensor_reduce(out=neg_max[:], in_=live[("scores", s)][:], axis=AX.X, op=ALU.max, negate=True)
+            live[("neg_max", s)] = neg_max
 
         def weights(s):
             e = work.tile([P, S], BF16, name="e", tag="e")
-            rs = small.tile([P, 1], F32, name="rs", tag="rs")
+            row_sum = small.tile([P, 1], F32, name="row_sum", tag="row_sum")
             nc.scalar.activation(
-                out=e[:], in_=st[("sc", s)][:], func=ACT.Exp, bias=st[("negm", s)][:], scale=1.0, accum_out=rs[:]
+                out=e[:], in_=live[("scores", s)][:], func=ACT.Exp, bias=live[("neg_max", s)][:], scale=1.0, accum_out=row_sum[:]
             )
-            st[("e", s)] = e
-            st[("rs", s)] = rs
+            live[("e", s)] = e
+            live[("row_sum", s)] = row_sum
 
         def flip(s):
-            e = st[("e", s)]
-            et = ps_et.tile([P, 2, 4, P], BF16, name="et", tag="et")
+            e = live[("e", s)]
+            e_t = ps_ring.tile([P, 2, PACK, P], BF16, name="e_t", tag="ring")
             for g in range(2):
-                for t in range(4):
-                    c0 = 512 * g + P * t
-                    nc.tensor.transpose(et[:, g, t, :], e[:, c0 : c0 + P], ident_b[:])
-            st[("et", s)] = et
+                for t in range(PACK):
+                    keys = slice(BANK * g + P * t, BANK * g + P * (t + 1))
+                    nc.tensor.transpose(e_t[:, g, t, :], e[:, keys], ident_b[:])
+            live[("e_t", s)] = e_t
 
         def regroup(s):
-            e_g = work.tile([P, 2, P, 4], BF16, name="e_g", tag="e_g", align_bytes=64)
-            nc.scalar.copy(out=e_g[:], in_=st[("et", s)][:].rearrange("p g t i -> p g i t"))
-            st[("e_g", s)] = e_g
+            e_grouped = work.tile([P, 2, P, PACK], BF16, name="e_grouped", tag="e_grouped", align_bytes=64)
+            nc.scalar.copy(out=e_grouped[:], in_=live[("e_t", s)][:].rearrange("p g t i -> p g i t"))
+            live[("e_grouped", s)] = e_grouped
 
-        def quantise_weights_of(s):
+        def quantise_e(s):
             e_codes = work.tile([P, 2 * P], U32, name="e_codes", tag="e_codes", align_bytes=64)
             e_scales = work.tile([P, 2 * P], U8, name="e_scales", tag="e_scales", align_bytes=64)
             nc.vector.quantize_mx(
                 out=e_codes[:].bitcast(FP8X4),
                 scales=e_scales[:],
-                in_=st[("e_g", s)][:].rearrange("p g i t -> p (g i t)"),
+                in_=live[("e_grouped", s)][:].rearrange("p g i t -> p (g i t)"),
             )
-            st[("mx", "e", s)] = (e_codes, e_scales)
-            rinv = small.tile([P, 1], F32, name="rinv", tag="rinv")
-            nc.vector.reciprocal(out=rinv[:], in_=st[("rs", s)][:])
-            st[("rinv", s)] = rinv
+            live[("mx", "e", s)] = (e_codes, e_scales)
+            inverse = small.tile([P, 1], F32, name="inverse", tag="inverse")
+            nc.vector.reciprocal(out=inverse[:], in_=live[("row_sum", s)][:])
+            live[("inverse", s)] = inverse
 
         def mix(s):
-            b, n = divmod(s, NT)
-            e_codes, e_scales = st[("mx", "e", s)]
-            v_codes, v_scales = st[("mx", "v", b)]
-            o_ps = ps_o.tile([P, D], F32, name="o_ps", tag="o")
+            e_codes, e_scales = live[("mx", "e", s)]
+            v_codes, v_scales = live[("mx", "v", s // NT)]
+            mixed = ps_ring.tile([P, D], F32, name="mixed", tag="ring")
             for g in range(2):
                 nc.tensor.matmul_mx(
-                    out=o_ps[:],
-                    lhsT=e_codes[:, P * g : P * g + P].bitcast(FP8X4),
-                    lhsT_scale=e_scales[:, P * g : P * g + P],
+                    out=mixed[:],
+                    lhsT=e_codes[:, P * g : P * (g + 1)].bitcast(FP8X4),
+                    lhsT_scale=e_scales[:, P * g : P * (g + 1)],
                     rhs=v_codes[:, g, :].bitcast(FP8X4),
                     rhs_scale=v_scales[:, g, :],
                     start=(g == 0),
                     stop=(g == 1),
                 )
-            st[("o", s)] = o_ps
+            live[("mixed", s)] = mixed
 
         def finish(s):
             b, n = divmod(s, NT)
-            rinv = st[("rinv", s)]
-            if n % 2 == 0:
-                st["o_sb"] = outp.tile([P, 2, D], F32, name="o_sb", tag="o_sb")
-            o_sb = st["o_sb"]
-            nc.vector.tensor_scalar_mul(out=o_sb[:, n % 2, :], in0=st[("o", s)][:], scalar1=rinv[:])
-            if n % 2 == 1:
-                nc.sync.dma_start(
-                    out=out[b].rearrange("(p n) d -> p n d", n=NT)[:, n - 1 : n + 1, :], in_=o_sb[:]
-                )
+            result = stores.tile([P, D], F32, name="result", tag="result")
+            nc.vector.tensor_scalar_mul(out=result[:], in0=live[("mixed", s)][:], scalar1=live[("inverse", s)][:])
+            nc.sync.dma_start(out=out[b].rearrange("(p n) d -> p n d", n=NT)[:, n, :], in_=result[:])
 
         def run(stage, s):
             if 0 <= s < STEPS:
                 stage(s)
 
-        def fills_of(s):
-            if s < START:
+
+        def units_of(s):
+            if s < FIRST_STEP:
                 return []
             b, n = divmod(s, NT)
-            bv_, j = divmod(s - 2, NT)
-            units = [(bv_ + 1, ("v", j))]
-            for unit in OTHERS[2 * n : 2 * n + 2]:
-                units.append((b + 2 if unit[0] == "x" else b + 1, unit))
-            return [(bb, unit) for bb, unit in units if 0 <= bb < B]
+            units = [((s - V_SHIFT) // NT + 1, ("v", (s - V_SHIFT) % NT))]
+            units += [(b + 2 if unit[0] == "x" else b + 1, unit) for unit in PAIRS[n]]
+            return [(batch, unit) for batch, unit in units if batch < B]
 
-        START = -2
-        LAG = 3
         load("k", 0)
         load("q", 0, (0,))
         load("x", 0)
@@ -349,49 +340,44 @@ def tile_selfattentionhybrid_pa_t_kernel(tc, q, k, x, Wv, bv, out):
         load("x", 1)
         load("k", 1)
         load("q", 1)
-        first = (
-            [("k", h) for h in range(4)]
-            + [("gram", 0), ("q", 0), ("q", 1), ("gram", 1)]
-            + [("x", h) for h in range(4)]
-            + [("kb", 0), ("kb", 1), ("q", 2), ("q", 3)]
-            + [("v", j) for j in range(4)]
-        )
-        for i in range(len(first) + LAG):
-            ready.extend(pending)
-            pending[:] = []
-            if i >= LAG:
-                drain(0, first[i - LAG], first[i - LAG][0] in ("k", "q", "x"))
-            if i < len(first):
-                fill(0, first[i])
-            quantise_pending()
-            if i == 14:
+
+        for i in range(len(PROLOGUE) + PROLOGUE_LAG):
+            next_round()
+            if i >= PROLOGUE_LAG:
+                unit = PROLOGUE[i - PROLOGUE_LAG]
+                drain(0, unit, unit[0] in ("k", "q", "x", "spread"))
+            if i < len(PROLOGUE):
+                fill(0, PROLOGUE[i])
+            quantise_ready()
+            if PROLOGUE[i : i + 1] == [("q", 2)]:
                 quantise_weights()
-            if 6 <= i < 20 and i % 2 == 0:
-                norm(0, (i - 6) // 2)
+            if i % 2 == 0 and 0 <= i // 2 - 3 < NT - 1:
+                query_norms(0, i // 2 - 3)
         load("x", 2)
-        for s in range(START, STEPS + 4):
+
+        for s in range(FIRST_STEP, STEPS + 5):
             b, n = divmod(s, NT)
             if n == 0 and s >= 0:
                 load("k", b + 2)
                 load("q", b + 2)
                 load("x", b + 3)
-            ready.extend(pending)
-            pending[:] = []
+            next_round()
             run(dots, s + 2)
             run(scores, s)
-            run(finish, s - 4)
-            for bb, unit in fills_of(s - 1):
-                drain(bb, unit, unit in (("k", 0), ("k", 2), ("x", 0), ("x", 2)) or unit[0] == "q")
-            for bb, unit in fills_of(s):
-                fill(bb, unit)
-            run(regroup, s - 2)
-            quantise_pending()
-            run(quantise_weights_of, s - 3)
-            run(mix, s - 3)
-            run(add_key_norms, s + 2)
+            for batch, unit in units_of(s - 1):
+                drain(batch, unit, unit == PAIRS[(s - 1) % NT][0])
+            for batch, unit in units_of(s)[:1]:
+                fill(batch, unit)
+            run(mix, s - 4)
+            for batch, unit in units_of(s)[1:]:
+                fill(batch, unit)
             run(weights, s - 1)
             run(flip, s - 1)
-            bq, m = divmod(s + 1, NT)
-            if 0 <= bq + 1 < B:
-                norm(bq + 1, m)
+            run(regroup, s - 2)
+            quantise_ready()
+            run(quantise_e, s - 3)
+            run(add_key_norms, s + 2)
+            run(finish, s - 4)
+            if (s + 1) // NT + 1 < B:
+                query_norms((s + 1) // NT + 1, (s + 1) % NT)
             run(row_max, s)

@@ -55,8 +55,6 @@ def tile_selfattentionhybrid_pa_t_kernel(tc, q, k, x, Wv, bv, out):
 
         ident_f = const.tile([P, P], F32, name="ident_f")
         make_identity(nc, ident_f[:])
-        ident_b = const.tile([P, P], BF16, name="ident_b")
-        make_identity(nc, ident_b[:])
         squares = const.tile([P, D], BF16, name="squares")
         ones_f = const.tile([P, P], F32, name="ones_f")
         nc.vector.memset(ones_f[:], 1.0)
@@ -188,8 +186,13 @@ def tile_selfattentionhybrid_pa_t_kernel(tc, q, k, x, Wv, bv, out):
                         opnd.tile([P, S], U8, name="scales_" + kind, tag="scales_" + kind, align_bytes=64),
                     )
                 tokens = live[("grouped", kind, b)]
-                dst = tokens[:].bitcast(F32)[:, 2 * P * j : 2 * P * (j + 1), :].rearrange("p (i r) u -> p i r u", i=2)
-                src = bank[:].rearrange("p (i u) r -> p i r u", u=2)
+                dst = tokens[:].bitcast(F32)[:, 2 * P * j : 2 * P * (j + 1), :]
+                if kind == "k":
+                    dst = dst.rearrange("p (r i) u -> p r i u", i=2)
+                    src = bank[:].rearrange("p (i u) r -> p r i u", u=2)
+                else:
+                    dst = dst.rearrange("p (i r) u -> p i r u", i=2)
+                    src = bank[:].rearrange("p (i u) r -> p i r u", u=2)
                 if on_scalar:
                     nc.scalar.copy(out=dst, in_=src)
                 else:
@@ -271,17 +274,18 @@ def tile_selfattentionhybrid_pa_t_kernel(tc, q, k, x, Wv, bv, out):
             live[("row_sum", s)] = row_sum
 
         def flip(s):
-            e = live[("e", s)]
-            e_t = ps_ring.tile([P, 2, PACK, P], BF16, name="e_t", tag="ring")
-            for g in range(2):
-                for t in range(PACK):
-                    keys = slice(BANK * g + P * t, BANK * g + P * (t + 1))
-                    nc.tensor.transpose(e_t[:, g, t, :], e[:, keys], ident_b[:])
+            words = live[("e", s)][:].bitcast(F32)
+            e_t = ps_ring.tile([P, 4, P], F32, name="e_t", tag="ring")
+            for i in range(4):
+                nc.tensor.transpose(e_t[:, i, :], words[:, P * i : P * (i + 1)], ident_f[:])
             live[("e_t", s)] = e_t
 
         def regroup(s):
-            e_grouped = work.tile([P, 2, P, PACK], BF16, name="e_grouped", tag="e_grouped", align_bytes=64)
-            nc.scalar.copy(out=e_grouped[:], in_=live[("e_t", s)][:].rearrange("p g t i -> p g i t"))
+            e_grouped = work.tile([P, 2 * P * PACK], BF16, name="e_grouped", tag="e_grouped", align_bytes=64)
+            nc.scalar.copy(
+                out=e_grouped[:].bitcast(F32).rearrange("p (g r u) -> p g r u", g=2, u=2),
+                in_=live[("e_t", s)][:].rearrange("p (g u) r -> p g r u", u=2),
+            )
             live[("e_grouped", s)] = e_grouped
 
         def quantise_e(s):
@@ -290,7 +294,7 @@ def tile_selfattentionhybrid_pa_t_kernel(tc, q, k, x, Wv, bv, out):
             nc.vector.quantize_mx(
                 out=e_codes[:].bitcast(FP8X4),
                 scales=e_scales[:],
-                in_=live[("e_grouped", s)][:].rearrange("p g i t -> p (g i t)"),
+                in_=live[("e_grouped", s)][:],
             )
             live[("mx", "e", s)] = (e_codes, e_scales)
             inverse = small.tile([P, 1], F32, name="inverse", tag="inverse")
@@ -365,7 +369,7 @@ def tile_selfattentionhybrid_pa_t_kernel(tc, q, k, x, Wv, bv, out):
             run(dots, s + 2)
             run(scores, s)
             for batch, unit in units_of(s - 1):
-                drain(batch, unit, unit == PAIRS[(s - 1) % NT][0])
+                drain(batch, unit, unit[0] in ("k", "q", "x", "spread"))
             for batch, unit in units_of(s)[:1]:
                 fill(batch, unit)
             run(mix, s - 4)

@@ -20,22 +20,41 @@ BANK = 512
 STEPS = B * NT
 FLOPS = 2 * B * S * D * D + 2 * 2 * B * S * S * D
 
-KEY_NORMS = [("gram", 0), ("gram", 1), ("spread", 0), ("spread", 1)]
-PAIRS = (
-    [(("k", 0), ("k", 1)), (("k", 2), ("k", 3))]
-    + [(("q", h), KEY_NORMS[h]) for h in range(4)]
-    + [(("x", 0), ("x", 1)), (("x", 2), ("x", 3))]
+GROUP = 4
+PLAIN = (
+    (("k", 0), ("k", 1), ("gram_q", 1)),
+    (("k", 2), ("k", 3)),
+    (("gram_k", 0), ("q", 0)),
+    (("gram_k", 1), ("q", 1)),
+    (("spread", 0), ("q", 2)),
+    (("spread", 1), ("q", 3), ("gram_q", 0)),
+    (("x", 0), ("x", 1)),
+    (("x", 2), ("x", 3)),
 )
-PROLOGUE = (
-    [("k", h) for h in range(4)]
-    + [("gram", 0), ("q", 0), ("q", 1), ("gram", 1)]
-    + [("x", h) for h in range(4)]
-    + [("spread", 0), ("spread", 1), ("q", 2), ("q", 3)]
-    + [("v", j) for j in range(4)]
-)
-PROLOGUE_LAG = 3
-FIRST_STEP = -2
 V_SHIFT = 2
+
+SCALAR, VECTOR = "scalar", "vector"
+HEAD = (
+    ("fill", ("k", 0)), ("fill", ("k", 1)), ("fill", ("k", 2)), ("fill", ("k", 3)),
+    ("drain", ("k", 0), VECTOR), ("square", "k", 0), ("square", "k", 1),
+    ("drain", ("k", 1), VECTOR), ("square", "k", 2), ("square", "k", 3),
+    ("drain", ("k", 2), VECTOR), ("quantise",), ("drain", ("k", 3), VECTOR),
+    ("square", "k", 4), ("square", "k", 5), ("square", "k", 6), ("square", "k", 7),
+    ("fill", ("q", 0)), ("fill", ("q", 1)), ("drain", ("q", 0), VECTOR), ("quantise",), ("drain", ("q", 1), VECTOR),
+    ("fill", ("spread", 0)), ("fill", ("spread", 1)), ("quantise",),
+    ("square", "q", 0), ("drain", ("spread", 0), SCALAR), ("square", "q", 1), ("drain", ("spread", 1), SCALAR),
+    ("weights",),
+    ("dots", 0), ("fill", ("x", 0)), ("fill", ("x", 1)),
+    ("square", "q", 2), ("square", "q", 3), ("add", 0),
+    ("drain", ("x", 0), SCALAR), ("dots", 1), ("fill", ("x", 2)), ("fill", ("x", 3)),
+    ("drain", ("x", 1), VECTOR), ("add", 1), ("drain", ("x", 2), VECTOR), ("drain", ("x", 3), SCALAR), ("quantise",),
+)
+OPENING = {
+    0: ((0, ("v", 0)), (0, ("v", 1)), (0, ("q", 2)), (0, ("q", 3))),
+    1: ((0, ("v", 2)), (0, ("v", 3)), (0, ("v", 4)), (1, ("x", 0)), (1, ("x", 1))),
+    2: ((0, ("v", 5)), (0, ("v", 6)), (0, ("v", 7)), (1, ("x", 2)), (1, ("x", 3))),
+    3: ((1, ("v", 0)),),
+}
 
 
 def tile_selfattentionhybrid_pa_t_kernel(tc, q, k, x, Wv, bv, out):
@@ -48,14 +67,14 @@ def tile_selfattentionhybrid_pa_t_kernel(tc, q, k, x, Wv, bv, out):
         grouped = ctx.enter_context(tc.tile_pool(name="grouped", bufs=3))
         work = ctx.enter_context(tc.tile_pool(name="work", bufs=4))
         small = ctx.enter_context(tc.tile_pool(name="small", bufs=4))
-        stores = ctx.enter_context(tc.tile_pool(name="stores", bufs=3))
+        stores = ctx.enter_context(tc.tile_pool(name="stores", bufs=6))
         ps_dots = ctx.enter_context(tc.psum_pool(name="ps_dots", bufs=2))
         ps_ring = ctx.enter_context(tc.psum_pool(name="ps_ring", bufs=6))
         ctx.enter_context(tc.manual_schedule())
 
         ident_f = const.tile([P, P], F32, name="ident_f")
         make_identity(nc, ident_f[:])
-        squares = const.tile([P, D], BF16, name="squares")
+        squares = const.tile([P, 2, D], BF16, name="squares")
         ones_f = const.tile([P, P], F32, name="ones_f")
         nc.vector.memset(ones_f[:], 1.0)
         wv_raw = const.tile([P, PACK, D], BF16, name="wv_raw")
@@ -69,14 +88,14 @@ def tile_selfattentionhybrid_pa_t_kernel(tc, q, k, x, Wv, bv, out):
         ready = []
 
 
-        def load(name, b, halves=(0, 1)):
+        def load(name, b, pieces=2, wanted=(0, 1)):
             if b < B:
-                if halves[0] == 0:
+                if wanted[0] == 0:
                     live[("raw", name, b)] = raw.tile([P, NT, D], BF16, name="raw_" + name, tag="raw_" + name)
                 rows = live[("raw", name, b)]
                 view = sources[name][b].rearrange("(p n) f -> p n f", n=NT)
-                for half in halves:
-                    tiles = slice(NT // 2 * half, NT // 2 * (half + 1))
+                for piece in wanted:
+                    tiles = slice(NT // pieces * piece, NT // pieces * (piece + 1))
                     nc.sync.dma_start(out=rows[:, tiles, :], in_=view[:, tiles, :])
 
         def load_weights():
@@ -99,14 +118,23 @@ def tile_selfattentionhybrid_pa_t_kernel(tc, q, k, x, Wv, bv, out):
         def fill(b, unit):
             kind, j = unit
             bank = ps_ring.tile([P, 4, P], F32, name="bank", tag="ring")
-            if kind == "gram":
-                k_t = live[("grouped", "k", b)]
+            if kind in ("gram_k", "gram_q"):
+                k_t = live[("grouped", kind[-1], b)]
                 for i in range(4):
                     cols = slice(P * (4 * j + i), P * (4 * j + i + 1))
                     for t in range(PACK):
                         nc.tensor.matmul(
                             bank[:, i, :], lhsT=k_t[:, cols, t], rhs=k_t[:, cols, t], start=(t == 0), stop=(t == PACK - 1)
                         )
+            elif kind == "spread" and b == 0:
+                for i in range(GROUP):
+                    nc.tensor.matmul(
+                        bank[:, i, :],
+                        lhsT=live[("squared", "k", j)][:, i : i + 1].to_broadcast([P, P]),
+                        rhs=ident_f[:],
+                        start=True,
+                        stop=True,
+                    )
             elif kind == "spread":
                 nc.tensor.matmul(
                     bank[:].rearrange("p a c -> p (a c)"),
@@ -140,7 +168,7 @@ def tile_selfattentionhybrid_pa_t_kernel(tc, q, k, x, Wv, bv, out):
         def drain(b, unit, on_scalar):
             kind, j = unit
             bank = live[("bank", b, unit)]
-            if kind == "gram":
+            if kind == "gram_k":
                 if j == 0:
                     live[("diagonal", b)] = opnd.tile([P, 2, BANK], F32, name="diagonal", tag="diagonal")
                 nc.vector.tensor_tensor(
@@ -149,11 +177,28 @@ def tile_selfattentionhybrid_pa_t_kernel(tc, q, k, x, Wv, bv, out):
                     in1=ident_f[:].unsqueeze(1).to_broadcast([P, 4, P]),
                     op=ALU.mult,
                 )
+            elif kind == "gram_q":
+                norms = small.tile([P, GROUP], F32, name="norms", tag="norms")
+                kept = small.tile([P, GROUP, P], BF16, name="kept", tag="kept")
+                for i in range(GROUP):
+                    nc.vector.scalar_tensor_tensor(
+                        out=kept[:, i, :],
+                        in0=bank[:, i, :],
+                        scalar=-1.0,
+                        in1=ident_f[:],
+                        op0=ALU.mult,
+                        op1=ALU.mult,
+                        accum_out=norms[:, i : i + 1],
+                    )
+                live[("norms", b, j)] = norms
             elif kind == "spread":
                 if j == 0:
                     live[("key_norms", b)] = opnd.tile([P, S], F32, name="key_norms", tag="key_norms")
                 dst = live[("key_norms", b)][:, BANK * j : BANK * (j + 1)]
                 src = bank[:].rearrange("p a c -> p (a c)")
+                if b == 0:
+                    dst = dst.rearrange("p (a r i) -> p a r i", a=2, i=2)
+                    src = bank[:].rearrange("p (a i) r -> p a r i", i=2)
                 if on_scalar:
                     nc.scalar.activation(out=dst, in_=src, func=ACT.Copy, scale=-0.5)
                 else:
@@ -211,17 +256,21 @@ def tile_selfattentionhybrid_pa_t_kernel(tc, q, k, x, Wv, bv, out):
                 nc.vector.quantize_mx(out=codes.bitcast(FP8X4), scales=scales, in_=src)
             ready[:] = []
 
-        def query_norms(b, n):
-            if n == 0:
-                live[("sums", b)] = opnd.tile([P, NT], F32, name="sums", tag="sums")
-            sums = live[("sums", b)]
+        def square(name, n):
+            j, column = divmod(n, GROUP)
+            if column == 0:
+                live[("squared", name, j)] = small.tile([P, GROUP], F32, name="squared_" + name, tag="squared_" + name)
+            sums = live[("squared", name, j)]
             nc.scalar.activation(
-                out=squares[:], in_=live[("raw", "q", b)][:, n, :], func=ACT.Square, accum_out=sums[:, n : n + 1]
+                out=squares[:, n % 2, :], in_=live[("raw", name, 0)][:, n, :], func=ACT.Square, accum_out=sums[:, column : column + 1]
             )
-            if n == NT - 1:
-                negated = opnd.tile([P, NT], F32, name="negated", tag="negated")
-                nc.scalar.activation(out=negated[:], in_=sums[:], func=ACT.Copy, scale=-1.0)
-                live[("query_norms", b)] = negated
+            if name == "q" and column == GROUP - 1:
+                norms = small.tile([P, GROUP], F32, name="norms", tag="norms")
+                nc.scalar.activation(out=norms[:], in_=sums[:], func=ACT.Copy, scale=-1.0)
+                live[("norms", 0, j)] = norms
+
+        def query_norm(b, n):
+            return live[("norms", b, n // GROUP)][:, n % GROUP : n % GROUP + 1]
 
 
         def dots(s):
@@ -255,7 +304,7 @@ def tile_selfattentionhybrid_pa_t_kernel(tc, q, k, x, Wv, bv, out):
             b, n = divmod(s, NT)
             sc = work.tile([P, S], F32, name="sc", tag="sc")
             nc.scalar.activation(
-                out=sc[:], in_=live[("half_d", s)][:], func=ACT.Exp, bias=live[("query_norms", b)][:, n : n + 1], scale=2.0
+                out=sc[:], in_=live[("half_d", s)][:], func=ACT.Exp, bias=query_norm(b, n), scale=2.0
             )
             live[("scores", s)] = sc
 
@@ -266,12 +315,13 @@ def tile_selfattentionhybrid_pa_t_kernel(tc, q, k, x, Wv, bv, out):
 
         def weights(s):
             e = work.tile([P, S], BF16, name="e", tag="e")
-            row_sum = small.tile([P, 1], F32, name="row_sum", tag="row_sum")
+            if s % 2 == 0:
+                live[("row_sums", s // 2)] = small.tile([P, 2], F32, name="row_sums", tag="row_sums")
+            row_sum = live[("row_sums", s // 2)][:, s % 2 : s % 2 + 1]
             nc.scalar.activation(
-                out=e[:], in_=live[("scores", s)][:], func=ACT.Exp, bias=live[("neg_max", s)][:], scale=1.0, accum_out=row_sum[:]
+                out=e[:], in_=live[("scores", s)][:], func=ACT.Exp, bias=live[("neg_max", s)][:], scale=1.0, accum_out=row_sum
             )
             live[("e", s)] = e
-            live[("row_sum", s)] = row_sum
 
         def flip(s):
             words = live[("e", s)][:].bitcast(F32)
@@ -297,9 +347,10 @@ def tile_selfattentionhybrid_pa_t_kernel(tc, q, k, x, Wv, bv, out):
                 in_=live[("e_grouped", s)][:],
             )
             live[("mx", "e", s)] = (e_codes, e_scales)
-            inverse = small.tile([P, 1], F32, name="inverse", tag="inverse")
-            nc.vector.reciprocal(out=inverse[:], in_=live[("row_sum", s)][:])
-            live[("inverse", s)] = inverse
+            if s % 2 == 1:
+                inverses = small.tile([P, 2], F32, name="inverses", tag="inverses")
+                nc.vector.reciprocal(out=inverses[:], in_=live[("row_sums", s // 2)][:])
+                live[("inverses", s // 2)] = inverses
 
         def mix(s):
             e_codes, e_scales = live[("mx", "e", s)]
@@ -320,7 +371,12 @@ def tile_selfattentionhybrid_pa_t_kernel(tc, q, k, x, Wv, bv, out):
         def finish(s):
             b, n = divmod(s, NT)
             result = stores.tile([P, D], F32, name="result", tag="result")
-            nc.vector.tensor_scalar_mul(out=result[:], in0=live[("mixed", s)][:], scalar1=live[("inverse", s)][:])
+            mixed = live[("mixed", s)]
+            inverse = live[("inverses", s // 2)][:, s % 2 : s % 2 + 1]
+            if n % 4 != 3 if b == B - 1 else n % 4 == 0:
+                nc.vector.tensor_scalar_mul(out=result[:], in0=mixed[:], scalar1=inverse)
+            else:
+                nc.scalar.activation(out=result[:], in_=mixed[:], func=ACT.Copy, scale=inverse)
             nc.sync.dma_start(out=out[b].rearrange("(p n) d -> p n d", n=NT)[:, n, :], in_=result[:])
 
         def run(stage, s):
@@ -329,59 +385,67 @@ def tile_selfattentionhybrid_pa_t_kernel(tc, q, k, x, Wv, bv, out):
 
 
         def units_of(s):
-            if s < FIRST_STEP:
+            if s < 0:
                 return []
             b, n = divmod(s, NT)
-            units = [((s - V_SHIFT) // NT + 1, ("v", (s - V_SHIFT) % NT))]
-            units += [(b + 2 if unit[0] == "x" else b + 1, unit) for unit in PAIRS[n]]
-            return [(batch, unit) for batch, unit in units if batch < B]
+            units = [] if s == V_SHIFT else [((s - V_SHIFT) // NT + 1, ("v", (s - V_SHIFT) % NT))]
+            units += [(b + {"x": 2}.get(unit[0], 0 if unit == ("gram_q", 1) else 1), unit) for unit in PLAIN[n]]
+            opening = list(OPENING.get(s, ()))
+            return [u for u in opening if u[1][0] == "v"] + [u for u in units if 0 < u[0] < B] + [u for u in opening if u[1][0] != "v"]
 
-        load("k", 0)
-        load("q", 0, (0,))
-        load("x", 0)
-        load("q", 0, (1,))
+        load("k", 0, 4, (0, 1, 2, 3))
+        load("q", 0, 2, (0,))
         load_weights()
+        load("x", 0)
+        load("q", 0, 2, (1,))
         load("x", 1)
         load("k", 1)
         load("q", 1)
 
-        for i in range(len(PROLOGUE) + PROLOGUE_LAG):
-            next_round()
-            if i >= PROLOGUE_LAG:
-                unit = PROLOGUE[i - PROLOGUE_LAG]
-                drain(0, unit, unit[0] in ("k", "q", "x", "spread"))
-            if i < len(PROLOGUE):
-                fill(0, PROLOGUE[i])
-            quantise_ready()
-            if PROLOGUE[i : i + 1] == [("q", 2)]:
+        for item in HEAD:
+            if item[0] == "fill":
+                fill(0, item[1])
+            elif item[0] == "drain":
+                drain(0, item[1], item[2] == SCALAR)
+            elif item[0] == "quantise":
+                next_round()
+                quantise_ready()
+            elif item[0] == "square":
+                square(item[1], item[2])
+            elif item[0] == "weights":
                 quantise_weights()
-            if i % 2 == 0 and 0 <= i // 2 - 3 < NT - 1:
-                query_norms(0, i // 2 - 3)
-        load("x", 2)
+            elif item[0] == "dots":
+                dots(item[1])
+            else:
+                add_key_norms(item[1])
 
-        for s in range(FIRST_STEP, STEPS + 5):
+        for s in range(STEPS + 5):
             b, n = divmod(s, NT)
-            if n == 0 and s >= 0:
+            if n == 0:
+                load("x", b + 2)
                 load("k", b + 2)
+            if n == 2:
                 load("q", b + 2)
-                load("x", b + 3)
             next_round()
+            quantise_ready()
             run(dots, s + 2)
             run(scores, s)
             for batch, unit in units_of(s - 1):
                 drain(batch, unit, unit[0] in ("k", "q", "x", "spread"))
-            for batch, unit in units_of(s)[:1]:
-                fill(batch, unit)
+            for batch, unit in units_of(s):
+                if unit[0] == "v":
+                    fill(batch, unit)
             run(mix, s - 4)
-            for batch, unit in units_of(s)[1:]:
-                fill(batch, unit)
+            run(flip, s - 2)
+            for batch, unit in units_of(s):
+                if unit[0] != "v":
+                    fill(batch, unit)
+            if s < 2:
+                for tile in range(4 + 2 * s, 6 + 2 * s):
+                    square("q", tile)
             run(weights, s - 1)
-            run(flip, s - 1)
             run(regroup, s - 2)
-            quantise_ready()
             run(quantise_e, s - 3)
             run(add_key_norms, s + 2)
             run(finish, s - 4)
-            if (s + 1) // NT + 1 < B:
-                query_norms((s + 1) // NT + 1, (s + 1) % NT)
             run(row_max, s)

@@ -41,9 +41,9 @@ HEAD = (
     ("drain", ("k", 2), VECTOR), ("quantise",), ("drain", ("k", 3), VECTOR),
     ("square", "k", 4), ("square", "k", 5), ("square", "k", 6), ("square", "k", 7),
     ("fill", ("q", 0)), ("fill", ("q", 1)), ("drain", ("q", 0), VECTOR), ("quantise",), ("drain", ("q", 1), VECTOR),
-    ("fill", ("spread", 0)), ("fill", ("spread", 1)), ("quantise",),
+    ("fill", ("spread", 0)), ("fill", ("spread", 1)), ("fill", ("bias", 0)), ("quantise",),
     ("square", "q", 0), ("drain", ("spread", 0), SCALAR), ("square", "q", 1), ("drain", ("spread", 1), SCALAR),
-    ("weights",),
+    ("weights",), ("drain", ("bias", 0), SCALAR),
     ("dots", 0), ("fill", ("x", 0)), ("fill", ("x", 1)),
     ("square", "q", 2), ("square", "q", 3), ("add", 0),
     ("drain", ("x", 0), SCALAR), ("dots", 1), ("fill", ("x", 2)), ("fill", ("x", 3)),
@@ -79,6 +79,10 @@ def tile_selfattentionhybrid_pa_t_kernel(tc, q, k, x, Wv, bv, out):
         nc.vector.memset(ones_f[:], 1.0)
         wv_raw = const.tile([P, PACK, D], BF16, name="wv_raw")
         bv_all = const.tile([P, D], BF16, name="bv_all")
+        bv_row = const.tile([P, D], BF16, name="bv_row")
+        nc.vector.memset(bv_row[:], 0.0)
+        ones_b = const.tile([P, P], BF16, name="ones_b")
+        nc.vector.memset(ones_b[:], 1.0)
         wv_grouped = const.tile([P, D, PACK], BF16, name="wv_grouped", align_bytes=64)
         wv_codes = const.tile([P, D], U32, name="wv_codes", align_bytes=64)
         wv_scales = const.tile([P, D], U8, name="wv_scales", align_bytes=64)
@@ -104,7 +108,6 @@ def tile_selfattentionhybrid_pa_t_kernel(tc, q, k, x, Wv, bv, out):
                     out=wv_raw[:, 2 * u : 2 * u + 2, :],
                     in_=Wv[256 * u : 256 * u + 256, :].rearrange("(r e) c -> r e c", e=2),
                 )
-            nc.gpsimd.dma_start(out=bv_all[:], in_=bv.partition_broadcast(P))
 
         def quantise_weights():
             nc.vector.tensor_copy(out=wv_grouped[:], in_=wv_raw[:].rearrange("p t c -> p c t"))
@@ -135,6 +138,8 @@ def tile_selfattentionhybrid_pa_t_kernel(tc, q, k, x, Wv, bv, out):
                         start=True,
                         stop=True,
                     )
+            elif kind == "bias":
+                nc.tensor.matmul(bank[:].rearrange("p a c -> p (a c)"), lhsT=ones_b[:], rhs=bv_row[:], start=True, stop=True)
             elif kind == "spread":
                 nc.tensor.matmul(
                     bank[:].rearrange("p a c -> p (a c)"),
@@ -191,6 +196,8 @@ def tile_selfattentionhybrid_pa_t_kernel(tc, q, k, x, Wv, bv, out):
                         accum_out=norms[:, i : i + 1],
                     )
                 live[("norms", b, j)] = norms
+            elif kind == "bias":
+                nc.scalar.copy(out=bv_all[:], in_=bank[:].rearrange("p a c -> p (a c)"))
             elif kind == "spread":
                 if j == 0:
                     live[("key_norms", b)] = opnd.tile([P, S], F32, name="key_norms", tag="key_norms")
@@ -394,6 +401,7 @@ def tile_selfattentionhybrid_pa_t_kernel(tc, q, k, x, Wv, bv, out):
             return [u for u in opening if u[1][0] == "v"] + [u for u in units if 0 < u[0] < B] + [u for u in opening if u[1][0] != "v"]
 
         load("k", 0, 4, (0, 1, 2, 3))
+        nc.sync.dma_start(out=bv_row[0:1, :], in_=bv.rearrange("(o c) -> o c", o=1))
         load("q", 0, 2, (0,))
         load_weights()
         load("x", 0)

@@ -22,13 +22,13 @@ FLOPS = 2 * B * S * D * D + 2 * 2 * B * S * S * D
 
 GROUP = 4
 PLAIN = (
-    (("k", 0), ("k", 1), ("gram_q", 1)),
-    (("k", 2), ("k", 3)),
+    (("k", 0), ("k", 1)),
+    (("k", 2), ("k", 3), ("gram_q", 1)),
     (("gram_k", 0), ("q", 0)),
     (("gram_k", 1), ("q", 1)),
     (("spread", 0), ("q", 2)),
-    (("spread", 1), ("q", 3), ("gram_q", 0)),
-    (("x", 0), ("x", 1)),
+    (("spread", 1), ("q", 3)),
+    (("x", 0), ("x", 1), ("gram_q", 0)),
     (("x", 2), ("x", 3)),
 )
 V_SHIFT = 2
@@ -380,7 +380,7 @@ def tile_selfattentionhybrid_pa_t_kernel(tc, q, k, x, Wv, bv, out):
             result = stores.tile([P, D], F32, name="result", tag="result")
             mixed = live[("mixed", s)]
             inverse = live[("inverses", s // 2)][:, s % 2 : s % 2 + 1]
-            if n % 4 != 3 if b == B - 1 else n % 4 == 0:
+            if n % 4 != 3 if b == B - 1 else b > 0 and n % 4 == 0:
                 nc.vector.tensor_scalar_mul(out=result[:], in0=mixed[:], scalar1=inverse)
             else:
                 nc.scalar.activation(out=result[:], in_=mixed[:], func=ACT.Copy, scale=inverse)

@@ -31,6 +31,7 @@ PLAIN = (
     (("x", 0), ("x", 1), ("gram_q", 0)),
     (("x", 2), ("x", 3)),
 )
+ORDER = ("dots", "flip", "mix", "v", "heavy", "light")
 V_SHIFT = 2
 
 SCALAR, VECTOR = "scalar", "vector"
@@ -131,13 +132,8 @@ def tile_selfattentionhybrid_pa_t_kernel(tc, q, k, x, Wv, bv, out):
                         )
             elif kind == "spread" and b == 0:
                 for i in range(GROUP):
-                    nc.tensor.matmul(
-                        bank[:, i, :],
-                        lhsT=live[("squared", "k", j)][:, i : i + 1].to_broadcast([P, P]),
-                        rhs=ident_f[:],
-                        start=True,
-                        stop=True,
-                    )
+                    column = live[("squared", "k", j)][:, i : i + 1]
+                    nc.tensor.transpose(bank[:, i, :], column.to_broadcast([P, P]), ident_f[:])
             elif kind == "bias":
                 nc.tensor.matmul(bank[:].rearrange("p a c -> p (a c)"), lhsT=ones_b[:], rhs=bv_row[:], start=True, stop=True)
             elif kind == "spread":
@@ -330,60 +326,84 @@ def tile_selfattentionhybrid_pa_t_kernel(tc, q, k, x, Wv, bv, out):
             )
             live[("e", s)] = e
 
-        def flip(s):
+        def flip(s, banks=1):
             words = live[("e", s)][:].bitcast(F32)
-            e_t = ps_ring.tile([P, 4, P], F32, name="e_t", tag="ring")
-            for i in range(4):
-                nc.tensor.transpose(e_t[:, i, :], words[:, P * i : P * (i + 1)], ident_f[:])
-            live[("e_t", s)] = e_t
+            per = 4 // banks
+            live[("e_t", s)] = []
+            for part in range(banks):
+                e_t = ps_ring.tile([P, per, P], F32, name="e_t", tag="ring")
+                for i in range(per):
+                    col = P * (per * part + i)
+                    nc.tensor.transpose(e_t[:, i, :], words[:, col : col + P], ident_f[:])
+                live[("e_t", s)].append(e_t)
+            live[("e_grouped", s)] = work.tile([P, 2 * P * PACK], BF16, name="e_grouped", tag="e_grouped", align_bytes=64)
 
-        def regroup(s):
-            e_grouped = work.tile([P, 2 * P * PACK], BF16, name="e_grouped", tag="e_grouped", align_bytes=64)
-            nc.scalar.copy(
-                out=e_grouped[:].bitcast(F32).rearrange("p (g r u) -> p g r u", g=2, u=2),
-                in_=live[("e_t", s)][:].rearrange("p (g u) r -> p g r u", u=2),
-            )
-            live[("e_grouped", s)] = e_grouped
+        def regroup(s, part=0, on_vector=False):
+            banks = live[("e_t", s)]
+            passes = 2 // len(banks)
+            words = slice(2 * P * passes * part, 2 * P * passes * (part + 1))
+            dst = live[("e_grouped", s)][:].bitcast(F32)[:, words].rearrange("p (g r u) -> p g r u", g=passes, u=2)
+            src = banks[part][:].rearrange("p (g u) r -> p g r u", u=2)
+            if on_vector:
+                nc.vector.tensor_copy(out=dst, in_=src)
+            else:
+                nc.scalar.copy(out=dst, in_=src)
 
-        def quantise_e(s):
-            e_codes = work.tile([P, 2 * P], U32, name="e_codes", tag="e_codes", align_bytes=64)
-            e_scales = work.tile([P, 2 * P], U8, name="e_scales", tag="e_scales", align_bytes=64)
+        def quantise_e(s, part=0, parts=1):
+            if part == 0:
+                live[("mx", "e", s)] = (
+                    work.tile([P, 2 * P], U32, name="e_codes", tag="e_codes", align_bytes=64),
+                    work.tile([P, 2 * P], U8, name="e_scales", tag="e_scales", align_bytes=64),
+                )
+            e_codes, e_scales = live[("mx", "e", s)]
+            width = 2 * P // parts
+            cols = slice(width * part, width * (part + 1))
             nc.vector.quantize_mx(
-                out=e_codes[:].bitcast(FP8X4),
-                scales=e_scales[:],
-                in_=live[("e_grouped", s)][:],
+                out=e_codes[:, cols].bitcast(FP8X4),
+                scales=e_scales[:, cols],
+                in_=live[("e_grouped", s)][:, PACK * width * part : PACK * width * (part + 1)],
             )
-            live[("mx", "e", s)] = (e_codes, e_scales)
-            if s % 2 == 1:
-                inverses = small.tile([P, 2], F32, name="inverses", tag="inverses")
-                nc.vector.reciprocal(out=inverses[:], in_=live[("row_sums", s // 2)][:])
-                live[("inverses", s // 2)] = inverses
+            if s % 2 == 1 and parts == 1:
+                invert(s)
 
-        def mix(s):
+        def invert(s):
+            inverses = small.tile([P, 2], F32, name="inverses", tag="inverses")
+            nc.vector.reciprocal(out=inverses[:], in_=live[("row_sums", s // 2)][:])
+            live[("inverses", s // 2)] = inverses
+
+        def mix(s, parts=1):
             e_codes, e_scales = live[("mx", "e", s)]
             v_codes, v_scales = live[("mx", "v", s // NT)]
-            mixed = ps_ring.tile([P, D], F32, name="mixed", tag="ring")
-            for g in range(2):
-                nc.tensor.matmul_mx(
-                    out=mixed[:],
-                    lhsT=e_codes[:, P * g : P * (g + 1)].bitcast(FP8X4),
-                    lhsT_scale=e_scales[:, P * g : P * (g + 1)],
-                    rhs=v_codes[:, g, :].bitcast(FP8X4),
-                    rhs_scale=v_scales[:, g, :],
-                    start=(g == 0),
-                    stop=(g == 1),
-                )
-            live[("mixed", s)] = mixed
+            width = D // parts
+            live[("mixed", s)] = []
+            for part in range(parts):
+                mixed = ps_ring.tile([P, width], F32, name="mixed", tag="ring")
+                for g in range(2):
+                    nc.tensor.matmul_mx(
+                        out=mixed[:],
+                        lhsT=e_codes[:, P * g : P * (g + 1)].bitcast(FP8X4),
+                        lhsT_scale=e_scales[:, P * g : P * (g + 1)],
+                        rhs=v_codes[:, g, width * part : width * (part + 1)].bitcast(FP8X4),
+                        rhs_scale=v_scales[:, g, width * part : width * (part + 1)],
+                        start=(g == 0),
+                        stop=(g == 1),
+                    )
+                live[("mixed", s)].append(mixed)
 
-        def finish(s):
+        def finish(s, on_vector=None):
             b, n = divmod(s, NT)
             result = stores.tile([P, D], F32, name="result", tag="result")
-            mixed = live[("mixed", s)]
             inverse = live[("inverses", s // 2)][:, s % 2 : s % 2 + 1]
-            if n % 4 != 3 if b == B - 1 else b > 0 and n % 4 == 0:
-                nc.vector.tensor_scalar_mul(out=result[:], in0=mixed[:], scalar1=inverse)
-            else:
-                nc.scalar.activation(out=result[:], in_=mixed[:], func=ACT.Copy, scale=inverse)
+            if on_vector is None:
+                on_vector = [n % 4 != 3 if b == B - 1 else b > 0 and n % 4 == 0]
+            width = D // len(on_vector)
+            for part, vector in enumerate(on_vector):
+                columns = slice(width * part, width * (part + 1))
+                mixed = live[("mixed", s)][part]
+                if vector:
+                    nc.vector.tensor_scalar_mul(out=result[:, columns], in0=mixed[:], scalar1=inverse)
+                else:
+                    nc.scalar.activation(out=result[:, columns], in_=mixed[:], func=ACT.Copy, scale=inverse)
             nc.sync.dma_start(out=out[b].rearrange("(p n) d -> p n d", n=NT)[:, n, :], in_=result[:])
 
         def run(stage, s):
@@ -427,7 +447,7 @@ def tile_selfattentionhybrid_pa_t_kernel(tc, q, k, x, Wv, bv, out):
             else:
                 add_key_norms(item[1])
 
-        for s in range(STEPS + 5):
+        for s in range(STEPS):
             b, n = divmod(s, NT)
             if n == 0:
                 load("x", b + 2)
@@ -436,24 +456,52 @@ def tile_selfattentionhybrid_pa_t_kernel(tc, q, k, x, Wv, bv, out):
                 load("q", b + 2)
             next_round()
             quantise_ready()
-            run(dots, s + 2)
             run(scores, s)
             for batch, unit in units_of(s - 1):
                 drain(batch, unit, unit[0] in ("k", "q", "x", "spread"))
-            for batch, unit in units_of(s):
-                if unit[0] == "v":
-                    fill(batch, unit)
-            run(mix, s - 4)
-            run(flip, s - 2)
-            for batch, unit in units_of(s):
-                if unit[0] != "v":
-                    fill(batch, unit)
+            for block in ORDER:
+                if block == "dots":
+                    run(dots, s + 2)
+                elif block == "mix":
+                    run(mix, s - 4)
+                elif block == "flip":
+                    run(flip, s - 2)
+                else:
+                    for batch, unit in units_of(s):
+                        if block == ("v" if unit[0] == "v" else "heavy" if unit[0] in ("gram_k", "gram_q", "spread") else "light"):
+                            fill(batch, unit)
             if s < 2:
                 for tile in range(4 + 2 * s, 6 + 2 * s):
                     square("q", tile)
             run(weights, s - 1)
-            run(regroup, s - 2)
+            if s < STEPS - 1:
+                run(regroup, s - 2)
             run(quantise_e, s - 3)
             run(add_key_norms, s + 2)
-            run(finish, s - 4)
+            if s < STEPS - 1:
+                run(finish, s - 4)
+            else:
+                finish(s - 4, [True])
             run(row_max, s)
+
+        z = STEPS - 1
+        regroup(z - 2)
+        flip(z - 1)
+        mix(z - 3)
+        weights(z)
+        quantise_e(z - 2)
+        regroup(z - 1, 0, True)
+        finish(z - 3, [False])
+        mix(z - 2)
+        flip(z, 2)
+        quantise_e(z - 1)
+        finish(z - 2, [True])
+        mix(z - 1)
+        invert(z)
+        regroup(z, 0, True)
+        regroup(z, 1, False)
+        quantise_e(z, 0, 2)
+        quantise_e(z, 1, 2)
+        finish(z - 1, [False])
+        mix(z, 2)
+        finish(z, [True, False])

from contextlib import ExitStack

import concourse.mybir as mybir
from concourse.masks import make_identity

F32 = mybir.dt.float32
BF16 = mybir.dt.bfloat16
U32 = mybir.dt.uint32
U8 = mybir.dt.uint8
FP8X4 = mybir.dt.float8_e4m3fn_x4
ACT = mybir.ActivationFunctionType
ALU = mybir.AluOpType
AX = mybir.AxisListType

B, S, D = 4, 1024, 512
P = 128
PACK = 4
NT = S // P
BANK = 512
STEPS = B * NT
FLOPS = 2 * B * S * D * D + 2 * 2 * B * S * S * D

GROUP = 4
PLAIN = (
    (("k", 0), ("k", 1)),
    (("k", 2), ("k", 3), ("gram_q", 1)),
    (("gram_k", 0), ("q", 0)),
    (("gram_k", 1), ("q", 1)),
    (("spread", 0), ("q", 2)),
    (("spread", 1), ("q", 3)),
    (("x", 0), ("x", 1), ("gram_q", 0)),
    (("x", 2), ("x", 3)),
)
ORDER = ("dots", "flip", "mix", "v", "heavy", "light")
V_SHIFT = 2

SCALAR, VECTOR = "scalar", "vector"
HEAD = (
    ("fill", ("k", 0)), ("fill", ("k", 1)), ("fill", ("k", 2)), ("fill", ("k", 3)),
    ("drain", ("k", 0), VECTOR), ("square", "k", 0), ("square", "k", 1),
    ("drain", ("k", 1), VECTOR), ("square", "k", 2), ("square", "k", 3),
    ("drain", ("k", 2), VECTOR), ("quantise",), ("drain", ("k", 3), VECTOR),
    ("square", "k", 4), ("square", "k", 5), ("square", "k", 6), ("square", "k", 7),
    ("fill", ("q", 0)), ("fill", ("q", 1)), ("drain", ("q", 0), VECTOR), ("quantise",), ("drain", ("q", 1), VECTOR),
    ("fill", ("spread", 0)), ("fill", ("spread", 1)), ("fill", ("bias", 0)), ("quantise",),
    ("square", "q", 0), ("drain", ("spread", 0), SCALAR), ("square", "q", 1), ("drain", ("spread", 1), SCALAR),
    ("weights",), ("drain", ("bias", 0), SCALAR),
    ("dots", 0), ("fill", ("x", 0)), ("fill", ("x", 1)),
    ("square", "q", 2), ("square", "q", 3), ("add", 0),
    ("drain", ("x", 0), SCALAR), ("dots", 1), ("fill", ("x", 2)), ("fill", ("x", 3)),
    ("drain", ("x", 1), VECTOR), ("add", 1), ("drain", ("x", 2), VECTOR), ("drain", ("x", 3), SCALAR), ("quantise",),
)
OPENING = {
    0: ((0, ("v", 0)), (0, ("v", 1)), (0, ("q", 2)), (0, ("q", 3))),
    1: ((0, ("v", 2)), (0, ("v", 3)), (0, ("v", 4)), (1, ("x", 0)), (1, ("x", 1))),
    2: ((0, ("v", 5)), (0, ("v", 6)), (0, ("v", 7)), (1, ("x", 2)), (1, ("x", 3))),
    3: ((1, ("v", 0)),),
}


def tile_selfattentionhybrid_pa_t_kernel(tc, q, k, x, Wv, bv, out):
    nc = tc.nc
    sources = {"k": k, "q": q, "x": x}
    with ExitStack() as ctx:
        const = ctx.enter_context(tc.tile_pool(name="const", bufs=1))
        raw = ctx.enter_context(tc.tile_pool(name="raw", bufs=2))
        opnd = ctx.enter_context(tc.tile_pool(name="opnd", bufs=2))
        grouped = ctx.enter_context(tc.tile_pool(name="grouped", bufs=3))
        work = ctx.enter_context(tc.tile_pool(name="work", bufs=4))
        small = ctx.enter_context(tc.tile_pool(name="small", bufs=4))
        stores = ctx.enter_context(tc.tile_pool(name="stores", bufs=6))
        ps_dots = ctx.enter_context(tc.psum_pool(name="ps_dots", bufs=2))
        ps_ring = ctx.enter_context(tc.psum_pool(name="ps_ring", bufs=6))
        ctx.enter_context(tc.manual_schedule())

        ident_f = const.tile([P, P], F32, name="ident_f")
        make_identity(nc, ident_f[:])
        squares = const.tile([P, 2, D], BF16, name="squares")
        ones_f = const.tile([P, P], F32, name="ones_f")
        nc.vector.memset(ones_f[:], 1.0)
        wv_raw = const.tile([P, PACK, D], BF16, name="wv_raw")
        bv_all = const.tile([P, D], BF16, name="bv_all")
        bv_row = const.tile([P, D], BF16, name="bv_row")
        nc.vector.memset(bv_row[:], 0.0)
        ones_b = const.tile([P, P], BF16, name="ones_b")
        nc.vector.memset(ones_b[:], 1.0)
        wv_grouped = const.tile([P, D, PACK], BF16, name="wv_grouped", align_bytes=64)
        wv_codes = const.tile([P, D], U32, name="wv_codes", align_bytes=64)
        wv_scales = const.tile([P, D], U8, name="wv_scales", align_bytes=64)

        live = {}
        drained = []
        ready = []


        def load(name, b, pieces=2, wanted=(0, 1)):
            if b < B:
                if wanted[0] == 0:
                    live[("raw", name, b)] = raw.tile([P, NT, D], BF16, name="raw_" + name, tag="raw_" + name)
                rows = live[("raw", name, b)]
                view = sources[name][b].rearrange("(p n) f -> p n f", n=NT)
                for piece in wanted:
                    tiles = slice(NT // pieces * piece, NT // pieces * (piece + 1))
                    nc.sync.dma_start(out=rows[:, tiles, :], in_=view[:, tiles, :])

        def load_weights():
            for u in range(2):
                nc.sync.dma_start(
                    out=wv_raw[:, 2 * u : 2 * u + 2, :],
                    in_=Wv[256 * u : 256 * u + 256, :].rearrange("(r e) c -> r e c", e=2),
                )

        def quantise_weights():
            nc.vector.tensor_copy(out=wv_grouped[:], in_=wv_raw[:].rearrange("p t c -> p c t"))
            nc.vector.quantize_mx(
                out=wv_codes[:].bitcast(FP8X4),
                scales=wv_scales[:],
                in_=wv_grouped[:].rearrange("p c t -> p (c t)"),
            )


        def fill(b, unit):
            kind, j = unit
            bank = ps_ring.tile([P, 4, P], F32, name="bank", tag="ring")
            if kind in ("gram_k", "gram_q"):
                k_t = live[("grouped", kind[-1], b)]
                for i in range(4):
                    cols = slice(P * (4 * j + i), P * (4 * j + i + 1))
                    for t in range(PACK):
                        nc.tensor.matmul(
                            bank[:, i, :], lhsT=k_t[:, cols, t], rhs=k_t[:, cols, t], start=(t == 0), stop=(t == PACK - 1)
                        )
            elif kind == "spread" and b == 0:
                for i in range(GROUP):
                    column = live[("squared", "k", j)][:, i : i + 1]
                    nc.tensor.transpose(bank[:, i, :], column.to_broadcast([P, P]), ident_f[:])
            elif kind == "bias":
                nc.tensor.matmul(bank[:].rearrange("p a c -> p (a c)"), lhsT=ones_b[:], rhs=bv_row[:], start=True, stop=True)
            elif kind == "spread":
                nc.tensor.matmul(
                    bank[:].rearrange("p a c -> p (a c)"),
                    lhsT=ones_f[:],
                    rhs=live[("diagonal", b)][:, j, :],
                    start=True,
                    stop=True,
                )
            elif kind == "v":
                g, dc = divmod(j, 4)
                x_codes, x_scales = live[("mx", "x", b)]
                for t in range(PACK):
                    keys = slice(BANK * g + P * t, BANK * g + P * (t + 1))
                    nc.tensor.matmul_mx(
                        out=bank[:, t, :],
                        lhsT=x_codes[:, keys].bitcast(FP8X4),
                        lhsT_scale=x_scales[:, keys],
                        rhs=wv_codes[:, P * dc : P * (dc + 1)].bitcast(FP8X4),
                        rhs_scale=wv_scales[:, P * dc : P * (dc + 1)],
                        start=True,
                        stop=True,
                    )
            else:
                rows = live[("raw", kind, b)]
                for i in range(2):
                    words = rows[:, 2 * j + i, :].bitcast(F32)
                    for u in range(2):
                        nc.tensor.transpose(bank[:, 2 * i + u, :], words[:, P * u : P * (u + 1)], ident_f[:])
            live[("bank", b, unit)] = bank

        def drain(b, unit, on_scalar):
            kind, j = unit
            bank = live[("bank", b, unit)]
            if kind == "gram_k":
                if j == 0:
                    live[("diagonal", b)] = opnd.tile([P, 2, BANK], F32, name="diagonal", tag="diagonal")
                nc.vector.tensor_tensor(
                    out=live[("diagonal", b)][:, j, :].rearrange("p (a c) -> p a c", a=4),
                    in0=bank[:],
                    in1=ident_f[:].unsqueeze(1).to_broadcast([P, 4, P]),
                    op=ALU.mult,
                )
            elif kind == "gram_q":
                norms = small.tile([P, GROUP], F32, name="norms", tag="norms")
                kept = small.tile([P, GROUP, P], BF16, name="kept", tag="kept")
                for i in range(GROUP):
                    nc.vector.scalar_tensor_tensor(
                        out=kept[:, i, :],
                        in0=bank[:, i, :],
                        scalar=-1.0,
                        in1=ident_f[:],
                        op0=ALU.mult,
                        op1=ALU.mult,
                        accum_out=norms[:, i : i + 1],
                    )
                live[("norms", b, j)] = norms
            elif kind == "bias":
                nc.scalar.copy(out=bv_all[:], in_=bank[:].rearrange("p a c -> p (a c)"))
            elif kind == "spread":
                if j == 0:
                    live[("key_norms", b)] = opnd.tile([P, S], F32, name="key_norms", tag="key_norms")
                dst = live[("key_norms", b)][:, BANK * j : BANK * (j + 1)]
                src = bank[:].rearrange("p a c -> p (a c)")
                if b == 0:
                    dst = dst.rearrange("p (a r i) -> p a r i", a=2, i=2)
                    src = bank[:].rearrange("p (a i) r -> p a r i", i=2)
                if on_scalar:
                    nc.scalar.activation(out=dst, in_=src, func=ACT.Copy, scale=-0.5)
                else:
                    nc.vector.tensor_scalar_mul(out=dst, in0=src, scalar1=-0.5)
            elif kind == "v":
                g, dc = divmod(j, 4)
                if j == 0:
                    live[("grouped", "v", b)] = opnd.tile([P, 2, D, PACK], BF16, name="v_grouped", tag="v_grouped", align_bytes=64)
                    live[("mx", "v", b)] = (
                        opnd.tile([P, 2, D], U32, name="v_codes", tag="v_codes", align_bytes=64),
                        opnd.tile([P, 2, D], U8, name="v_scales", tag="v_scales", align_bytes=64),
                    )
                v_grouped = live[("grouped", "v", b)]
                nc.vector.tensor_tensor(
                    out=v_grouped[:, g, P * dc : P * (dc + 1), :],
                    in0=bank[:].rearrange("p t d -> p d t"),
                    in1=bv_all[:, P * dc : P * (dc + 1)].unsqueeze(2).to_broadcast([P, P, PACK]),
                    op=ALU.add,
                )
                if dc == 3:
                    v_codes, v_scales = live[("mx", "v", b)]
                    drained.append(
                        (v_codes[:, g, :], v_scales[:, g, :], v_grouped[:, g, :, :].rearrange("p d t -> p (d t)"))
                    )
            else:
                if j == 0:
                    live[("grouped", kind, b)] = grouped.tile([P, S, PACK], BF16, name="grouped_" + kind, tag="grouped", align_bytes=64)
                    live[("mx", kind, b)] = (
                        opnd.tile([P, S], U32, name="codes_" + kind, tag="codes_" + kind, align_bytes=64),
                        opnd.tile([P, S], U8, name="scales_" + kind, tag="scales_" + kind, align_bytes=64),
                    )
                tokens = live[("grouped", kind, b)]
                dst = tokens[:].bitcast(F32)[:, 2 * P * j : 2 * P * (j + 1), :]
                if kind == "k":
                    dst = dst.rearrange("p (r i) u -> p r i u", i=2)
                    src = bank[:].rearrange("p (i u) r -> p r i u", u=2)
                else:
                    dst = dst.rearrange("p (i r) u -> p i r u", i=2)
                    src = bank[:].rearrange("p (i u) r -> p i r u", u=2)
                if on_scalar:
                    nc.scalar.copy(out=dst, in_=src)
                else:
                    nc.vector.tensor_copy(out=dst, in_=src)
                if j % 2 == 1:
                    half = slice(BANK * (j // 2), BANK * (j // 2 + 1))
                    codes, scales = live[("mx", kind, b)]
                    drained.append((codes[:, half], scales[:, half], tokens[:, half, :].rearrange("p c t -> p (c t)")))

        def next_round():
            ready.extend(drained)
            drained[:] = []

        def quantise_ready():
            for codes, scales, src in ready:
                nc.vector.quantize_mx(out=codes.bitcast(FP8X4), scales=scales, in_=src)
            ready[:] = []

        def square(name, n):
            j, column = divmod(n, GROUP)
            if column == 0:
                live[("squared", name, j)] = small.tile([P, GROUP], F32, name="squared_" + name, tag="squared_" + name)
            sums = live[("squared", name, j)]
            nc.scalar.activation(
                out=squares[:, n % 2, :], in_=live[("raw", name, 0)][:, n, :], func=ACT.Square, accum_out=sums[:, column : column + 1]
            )
            if name == "q" and column == GROUP - 1:
                norms = small.tile([P, GROUP], F32, name="norms", tag="norms")
                nc.scalar.activation(out=norms[:], in_=sums[:], func=ACT.Copy, scale=-1.0)
                live[("norms", 0, j)] = norms

        def query_norm(b, n):
            return live[("norms", b, n // GROUP)][:, n % GROUP : n % GROUP + 1]


        def dots(s):
            b, n = divmod(s, NT)
            q_codes, q_scales = live[("mx", "q", b)]
            k_codes, k_scales = live[("mx", "k", b)]
            banks = []
            for h in range(2):
                bank = ps_dots.tile([P, BANK], F32, name="dots", tag="dots")
                nc.tensor.matmul_mx(
                    out=bank[:],
                    lhsT=q_codes[:, P * n : P * (n + 1)].bitcast(FP8X4),
                    lhsT_scale=q_scales[:, P * n : P * (n + 1)],
                    rhs=k_codes[:, BANK * h : BANK * (h + 1)].bitcast(FP8X4),
                    rhs_scale=k_scales[:, BANK * h : BANK * (h + 1)],
                    start=True,
                    stop=True,
                )
                banks.append(bank)
            live[("dots", s)] = banks

        def add_key_norms(s):
            key_norms = live[("key_norms", s // NT)]
            half_d = work.tile([P, S], F32, name="half_d", tag="half_d")
            for h in range(2):
                cols = slice(BANK * h, BANK * (h + 1))
                nc.vector.tensor_tensor(out=half_d[:, cols], in0=live[("dots", s)][h][:], in1=key_norms[:, cols], op=ALU.add)
            live[("half_d", s)] = half_d

        def scores(s):
            b, n = divmod(s, NT)
            sc = work.tile([P, S], F32, name="sc", tag="sc")
            nc.scalar.activation(
                out=sc[:], in_=live[("half_d", s)][:], func=ACT.Exp, bias=query_norm(b, n), scale=2.0
            )
            live[("scores", s)] = sc

        def row_max(s):
            neg_max = small.tile([P, 1], F32, name="neg_max", tag="neg_max")
            nc.vector.tensor_reduce(out=neg_max[:], in_=live[("scores", s)][:], axis=AX.X, op=ALU.max, negate=True)
            live[("neg_max", s)] = neg_max

        def weights(s):
            e = work.tile([P, S], BF16, name="e", tag="e")
            if s % 2 == 0:
                live[("row_sums", s // 2)] = small.tile([P, 2], F32, name="row_sums", tag="row_sums")
            row_sum = live[("row_sums", s // 2)][:, s % 2 : s % 2 + 1]
            nc.scalar.activation(
                out=e[:], in_=live[("scores", s)][:], func=ACT.Exp, bias=live[("neg_max", s)][:], scale=1.0, accum_out=row_sum
            )
            live[("e", s)] = e

        def flip(s, banks=1):
            words = live[("e", s)][:].bitcast(F32)
            per = 4 // banks
            live[("e_t", s)] = []
            for part in range(banks):
                e_t = ps_ring.tile([P, per, P], F32, name="e_t", tag="ring")
                for i in range(per):
                    col = P * (per * part + i)
                    nc.tensor.transpose(e_t[:, i, :], words[:, col : col + P], ident_f[:])
                live[("e_t", s)].append(e_t)
            live[("e_grouped", s)] = work.tile([P, 2 * P * PACK], BF16, name="e_grouped", tag="e_grouped", align_bytes=64)

        def regroup(s, part=0, on_vector=False):
            banks = live[("e_t", s)]
            passes = 2 // len(banks)
            words = slice(2 * P * passes * part, 2 * P * passes * (part + 1))
            dst = live[("e_grouped", s)][:].bitcast(F32)[:, words].rearrange("p (g r u) -> p g r u", g=passes, u=2)
            src = banks[part][:].rearrange("p (g u) r -> p g r u", u=2)
            if on_vector:
                nc.vector.tensor_copy(out=dst, in_=src)
            else:
                nc.scalar.copy(out=dst, in_=src)

        def quantise_e(s, part=0, parts=1):
            if part == 0:
                live[("mx", "e", s)] = (
                    work.tile([P, 2 * P], U32, name="e_codes", tag="e_codes", align_bytes=64),
                    work.tile([P, 2 * P], U8, name="e_scales", tag="e_scales", align_bytes=64),
                )
            e_codes, e_scales = live[("mx", "e", s)]
            width = 2 * P // parts
            cols = slice(width * part, width * (part + 1))
            nc.vector.quantize_mx(
                out=e_codes[:, cols].bitcast(FP8X4),
                scales=e_scales[:, cols],
                in_=live[("e_grouped", s)][:, PACK * width * part : PACK * width * (part + 1)],
            )
            if s % 2 == 1 and parts == 1:
                invert(s)

        def invert(s):
            inverses = small.tile([P, 2], F32, name="inverses", tag="inverses")
            nc.vector.reciprocal(out=inverses[:], in_=live[("row_sums", s // 2)][:])
            live[("inverses", s // 2)] = inverses

        def mix(s, parts=1):
            e_codes, e_scales = live[("mx", "e", s)]
            v_codes, v_scales = live[("mx", "v", s // NT)]
            width = D // parts
            live[("mixed", s)] = []
            for part in range(parts):
                mixed = ps_ring.tile([P, width], F32, name="mixed", tag="ring")
                for g in range(2):
                    nc.tensor.matmul_mx(
                        out=mixed[:],
                        lhsT=e_codes[:, P * g : P * (g + 1)].bitcast(FP8X4),
                        lhsT_scale=e_scales[:, P * g : P * (g + 1)],
                        rhs=v_codes[:, g, width * part : width * (part + 1)].bitcast(FP8X4),
                        rhs_scale=v_scales[:, g, width * part : width * (part + 1)],
                        start=(g == 0),
                        stop=(g == 1),
                    )
                live[("mixed", s)].append(mixed)

        def finish(s, on_vector=None):
            b, n = divmod(s, NT)
            result = stores.tile([P, D], F32, name="result", tag="result")
            inverse = live[("inverses", s // 2)][:, s % 2 : s % 2 + 1]
            if on_vector is None:
                on_vector = [n % 4 != 3 if b == B - 1 else b > 0 and n % 4 == 0]
            width = D // len(on_vector)
            for part, vector in enumerate(on_vector):
                columns = slice(width * part, width * (part + 1))
                mixed = live[("mixed", s)][part]
                if vector:
                    nc.vector.tensor_scalar_mul(out=result[:, columns], in0=mixed[:], scalar1=inverse)
                else:
                    nc.scalar.activation(out=result[:, columns], in_=mixed[:], func=ACT.Copy, scale=inverse)
            nc.sync.dma_start(out=out[b].rearrange("(p n) d -> p n d", n=NT)[:, n, :], in_=result[:])

        def run(stage, s):
            if 0 <= s < STEPS:
                stage(s)


        def units_of(s):
            if s < 0:
                return []
            b, n = divmod(s, NT)
            units = [] if s == V_SHIFT else [((s - V_SHIFT) // NT + 1, ("v", (s - V_SHIFT) % NT))]
            units += [(b + {"x": 2}.get(unit[0], 0 if unit == ("gram_q", 1) else 1), unit) for unit in PLAIN[n]]
            opening = list(OPENING.get(s, ()))
            return [u for u in opening if u[1][0] == "v"] + [u for u in units if 0 < u[0] < B] + [u for u in opening if u[1][0] != "v"]

        load("k", 0, 4, (0, 1, 2, 3))
        nc.sync.dma_start(out=bv_row[0:1, :], in_=bv.rearrange("(o c) -> o c", o=1))
        load("q", 0, 2, (0,))
        load_weights()
        load("x", 0)
        load("q", 0, 2, (1,))
        load("x", 1)
        load("k", 1)
        load("q", 1)

        for item in HEAD:
            if item[0] == "fill":
                fill(0, item[1])
            elif item[0] == "drain":
                drain(0, item[1], item[2] == SCALAR)
            elif item[0] == "quantise":
                next_round()
                quantise_ready()
            elif item[0] == "square":
                square(item[1], item[2])
            elif item[0] == "weights":
                quantise_weights()
            elif item[0] == "dots":
                dots(item[1])
            else:
                add_key_norms(item[1])

        for s in range(STEPS):
            b, n = divmod(s, NT)
            if n == 0:
                load("x", b + 2)
                load("k", b + 2)
            if n == 2:
                load("q", b + 2)
            next_round()
            quantise_ready()
            run(scores, s)
            for batch, unit in units_of(s - 1):
                drain(batch, unit, unit[0] in ("k", "q", "x", "spread"))
            for block in ORDER:
                if block == "dots":
                    run(dots, s + 2)
                elif block == "mix":
                    run(mix, s - 4)
                elif block == "flip":
                    run(flip, s - 2)
                else:
                    for batch, unit in units_of(s):
                        if block == ("v" if unit[0] == "v" else "heavy" if unit[0] in ("gram_k", "gram_q", "spread") else "light"):
                            fill(batch, unit)
            if s < 2:
                for tile in range(4 + 2 * s, 6 + 2 * s):
                    square("q", tile)
            run(weights, s - 1)
            if s < STEPS - 1:
                run(regroup, s - 2)
            run(quantise_e, s - 3)
            run(add_key_norms, s + 2)
            if s < STEPS - 1:
                run(finish, s - 4)
            else:
                finish(s - 4, [True])
            run(row_max, s)

        z = STEPS - 1
        regroup(z - 2)
        flip(z - 1)
        mix(z - 3)
        weights(z)
        quantise_e(z - 2)
        regroup(z - 1, 0, True)
        finish(z - 3, [False])
        mix(z - 2)
        flip(z, 2)
        quantise_e(z - 1)
        finish(z - 2, [True])
        mix(z - 1)
        invert(z)
        regroup(z, 0, True)
        regroup(z, 1, False)
        quantise_e(z, 0, 2)
        quantise_e(z, 1, 2)
        finish(z - 1, [False])
        mix(z, 2)
        finish(z, [True, False])
